import numpy as np
import ml_dtypes


def mxq(x, axis, fmt="e4m3"):
    dtype, down = {"e4m3": (ml_dtypes.float8_e4m3fn, 7), "e5m2": (ml_dtypes.float8_e5m2, 14)}[fmt]
    v = np.moveaxis(np.asarray(x, np.float32).astype(ml_dtypes.bfloat16).astype(np.float64), axis, -1)
    blocks = v.reshape(v.shape[:-1] + (-1, 32))
    amax = np.abs(blocks).max(-1, keepdims=True)
    byte = np.maximum(np.where(amax > 0, np.frexp(amax)[1] - 1 + 127, 0) - down, 1)
    scale = np.exp2(byte - 127.0)
    codes = (blocks / scale).astype(np.float32).astype(dtype).astype(np.float64)
    return np.moveaxis((codes * scale).reshape(v.shape), -1, axis)


WIDE = False


def mx_kscale(k):
    if not WIDE:
        return np.ones(k)
    levels = np.array([10, -10, 5, -5, 0])
    a = np.random.permutation(np.resize(levels, k // 512 * 4)).reshape(k // 512, 4)
    idx = np.arange(k)
    return np.exp2(a[idx // 512, idx % 128 // 32])


BF16 = ml_dtypes.bfloat16


def bf(x):
    return np.asarray(x, np.float32).astype(BF16)


def f64(x):
    return np.asarray(x).astype(np.float64)


B, S, C, MID = 2, 4096, 256, 512
K0 = 2 * C


def gelu_tanh(v):
    return 0.5 * v * (1.0 + np.tanh(np.sqrt(2.0 / np.pi) * (v + 0.044715 * v**3)))


def setup_inputs():
    u = mx_kscale(K0)[:C]
    uu = np.concatenate([u, u])
    return {"sample_features": bf(np.random.standard_normal((B, S, C)) * u),
            "query_samples": bf(np.random.standard_normal((B, S, C)) * u),
            "pos_enc": bf(np.random.standard_normal((B, S, C)) * u),
            "W0": bf(np.random.standard_normal((K0, MID)) * 0.6 / np.sqrt(K0) / uu[:, None]),
            "b0": bf(np.random.standard_normal(MID) * 0.2),
            "W1": bf(np.random.standard_normal((MID, MID)) * 1.5 / np.sqrt(MID)),
            "b1": bf(np.random.standard_normal(MID) * 0.2)}


def reference(sample_features, query_samples, pos_enc, W0, b0, W1, b1):
    sf = f64(sample_features)
    q = f64(query_samples) + f64(pos_enc)
    x = np.concatenate([sf - q, q], axis=-1)
    h = gelu_tanh((mxq(x, 2, "e4m3") @ mxq(f64(W0), 0, "e4m3")) + f64(b0))
    return gelu_tanh((mxq(h, 2, "e4m3") @ mxq(f64(W1), 0, "e4m3")) + f64(b1))

@@ -1,0 +1,196 @@
+from contextlib import ExitStack
+
+import concourse.mybir as mybir
+from concourse.masks import make_identity
+
+F32 = mybir.dt.float32
+BF16 = mybir.dt.bfloat16
+U32 = mybir.dt.uint32
+U8 = mybir.dt.uint8
+FP8X4 = mybir.dt.float8_e4m3fn_x4
+ALU = mybir.AluOpType
+ACT = mybir.ActivationFunctionType
+
+P = 128
+PACK = 4
+TOKENS = 2 * 4096
+C = 256
+MID = 512
+ROWS = TOKENS // P
+UNIT_ROWS = 4
+UNIT = UNIT_ROWS * P
+UNITS = ROWS // UNIT_ROWS
+CHUNK_ROWS = 8
+HALF = UNIT // 2
+SAMPLE_BUFS = 2
+
+FLOPS = 2 * TOKENS * (2 * C * MID + MID * MID)
+
+
+def quantise_weight(nc, stage, keep, weight, negated, name):
+    raw = stage.tile([P, PACK, MID], BF16, name=name + "_raw")
+    nc.sync.dma_start(out=raw[:], in_=weight.rearrange("(t p) n -> p t n", p=P))
+    if negated:
+        nc.vector.tensor_scalar_mul(out=raw[:, PACK - negated :, :], in0=raw[:, PACK - negated :, :], scalar1=-1.0)
+    grouped = stage.tile([P, MID, PACK], BF16, name=name + "_grouped", align_bytes=64)
+    nc.vector.tensor_copy(out=grouped[:], in_=raw[:].rearrange("p t n -> p n t"))
+    codes = keep.tile([P, MID], U32, name=name + "_codes", align_bytes=64)
+    scales = keep.tile([P, MID], U8, name=name + "_scales", align_bytes=64)
+    nc.vector.quantize_mx(
+        out=codes[:].bitcast(FP8X4),
+        scales=scales[:],
+        in_=grouped[:].rearrange("p n t -> p (n t)"),
+    )
+    return codes, scales
+
+
+def tile_samplequerymessagepassing_pa_t_kernel(
+    tc, sample_features, query_samples, pos_enc, W0, b0, W1, b1, out
+):
+    nc = tc.nc
+    sample_rows = sample_features.rearrange("b s c -> (b s) c").rearrange("(p r) c -> p (r c)", p=P)
+    out_rows = out.rearrange("b s m -> (b s) m").rearrange("(p r) m -> p r m", p=P)
+    query_rows = query_samples.rearrange("b s c -> (b s) c").rearrange("(a n r) c -> n a (r c)", a=2, r=ROWS)
+    pos_rows = pos_enc.rearrange("b s c -> (b s) c").rearrange("(a n r) c -> n a (r c)", a=2, r=ROWS)
+
+    with ExitStack() as ctx:
+        keep = ctx.enter_context(tc.tile_pool(name="keep", bufs=1))
+        stage = ctx.enter_context(tc.tile_pool(name="stage", bufs=1))
+        loads = ctx.enter_context(tc.tile_pool(name="loads", bufs=3))
+        work = ctx.enter_context(tc.tile_pool(name="work", bufs=2))
+        stores = ctx.enter_context(tc.tile_pool(name="stores", bufs=3))
+        ps_sample = ctx.enter_context(tc.psum_pool(name="ps_sample", bufs=1))
+        ps_q = ctx.enter_context(tc.psum_pool(name="ps_q", bufs=2))
+        ps_h = ctx.enter_context(tc.psum_pool(name="ps_h", bufs=3))
+        ps_out = ctx.enter_context(tc.psum_pool(name="ps_out", bufs=2))
+
+        ident = keep.tile([P, P], BF16)
+        make_identity(nc, ident[:])
+        add_pairs = keep.tile([P, P // 2], BF16)
+        ident_pairs = ident[:].rearrange("k (n j) -> k n j", j=2)
+        nc.vector.tensor_tensor(out=add_pairs[:], in0=ident_pairs[:, :, 0], in1=ident_pairs[:, :, 1], op=ALU.add)
+
+        sample_t = []
+        for i in range(SAMPLE_BUFS):
+            sample_zero = keep.tile([P, 2, 2, UNIT], BF16, name="sample_zero%d" % i)
+            nc.vector.memset(sample_zero[:, 1, :, :], 0.0)
+            sample_t.append(sample_zero)
+
+        w0_codes, w0_scales = quantise_weight(nc, stage, keep, W0, 2, "w0")
+        w1_codes, w1_scales = quantise_weight(nc, stage, keep, W1, 0, "w1")
+
+        b0_rows = stage.tile([P, P], BF16)
+        nc.vector.memset(b0_rows[:], 0.0)
+        nc.sync.dma_start(out=b0_rows[0:PACK, :], in_=b0.rearrange("(m p) -> m p", p=P))
+        b0_ps = ps_sample.tile([P, P], BF16, tag="sample_ps")
+        nc.tensor.transpose(b0_ps[:], b0_rows[:], ident[:])
+        b0_cols = keep.tile([P, PACK], F32)
+        nc.vector.tensor_copy(out=b0_cols[:], in_=b0_ps[:, 0:PACK])
+
+        b1_bf16 = stage.tile([P, MID], BF16)
+        nc.sync.dma_start(out=b1_bf16[:], in_=b1.partition_broadcast(P))
+        b1_all = keep.tile([P, MID], F32)
+        nc.vector.tensor_copy(out=b1_all[:], in_=b1_bf16[:])
+
+        chunk = {}
+        for unit in range(UNITS):
+            row0 = unit * UNIT_ROWS
+            if row0 % CHUNK_ROWS == 0:
+                cols = slice(row0 * C, (row0 + CHUNK_ROWS) * C)
+                query_pos = loads.tile([P, 2, CHUNK_ROWS * C], BF16)
+                nc.sync.dma_start(out=query_pos[0:P:2, :, :], in_=query_rows[:, :, cols])
+                nc.sync.dma_start(out=query_pos[1:P:2, :, :], in_=pos_rows[:, :, cols])
+                sample_sb = loads.tile([P, CHUNK_ROWS * C], BF16)
+                nc.sync.dma_start(out=sample_sb[:], in_=sample_rows[:, cols])
+                chunk = {"query_pos": query_pos, "sample": sample_sb}
+
+            sample_ps = ps_sample.tile([P, 2, UNIT], BF16, tag="sample_ps")
+            q_banks = []
+            for half in range(2):
+                q_ps = ps_q.tile([P, 2, HALF], F32)
+                q_banks.append(q_ps)
+            for j in range(UNIT_ROWS):
+                for c in range(2):
+                    first = ((row0 % CHUNK_ROWS) + j) * C + c * P
+                    nc.tensor.transpose(
+                        sample_ps[:, c, j * P : (j + 1) * P], chunk["sample"][:, first : first + P], ident[:]
+                    )
+                    for a in range(2):
+                        n0 = (j % 2) * P + a * (P // 2)
+                        nc.tensor.matmul(
+                            out=q_banks[j // 2][:, c, n0 : n0 + P // 2],
+                            lhsT=chunk["query_pos"][:, a, first : first + P],
+                            rhs=add_pairs[:],
+                            start=True,
+                            stop=True,
+                        )
+            sample_zero = sample_t[unit % SAMPLE_BUFS]
+            nc.scalar.copy(out=sample_zero[:, 0, :, :], in_=sample_ps[:])
+
+            x_grouped = work.tile([P, UNIT, PACK], BF16, align_bytes=64)
+            for half in range(2):
+                tokens = slice(half * HALF, (half + 1) * HALF)
+                nc.vector.tensor_tensor(
+                    out=x_grouped[:, tokens, :].rearrange("p n (u c) -> p n u c", c=2),
+                    in0=sample_zero[:, :, :, tokens].rearrange("p u c n -> p n u c"),
+                    in1=q_banks[half][:].rearrange("p c n -> p n c").unsqueeze(2).to_broadcast([P, HALF, 2, 2]),
+                    op=ALU.subtract,
+                )
+            x_codes = work.tile([P, UNIT], U32, align_bytes=64)
+            x_scales = work.tile([P, UNIT], U8, align_bytes=64)
+            nc.vector.quantize_mx(
+                out=x_codes[:].bitcast(FP8X4),
+                scales=x_scales[:],
+                in_=x_grouped[:].rearrange("p n t -> p (n t)"),
+            )
+
+            h_planes = work.tile([P, PACK, UNIT], BF16)
+            for m in range(PACK):
+                m_cols = slice(m * P, (m + 1) * P)
+                h_ps = ps_h.tile([P, UNIT], F32)
+                nc.tensor.matmul_mx(
+                    out=h_ps[:],
+                    lhsT=w0_codes[:, m_cols].bitcast(FP8X4),
+                    lhsT_scale=w0_scales[:, m_cols],
+                    rhs=x_codes[:].bitcast(FP8X4),
+                    rhs_scale=x_scales[:],
+                    start=True,
+                    stop=True,
+                )
+                nc.scalar.activation(
+                    out=h_planes[:, m, :], in_=h_ps[:], func=ACT.Gelu_apprx_tanh, bias=b0_cols[:, m : m + 1], scale=1.0
+                )
+            h_grouped = work.tile([P, UNIT, PACK], BF16, align_bytes=64)
+            nc.gpsimd.tensor_scalar(
+                out=h_grouped[:],
+                in0=h_planes[:].rearrange("p t n -> p n t"),
+                scalar1=1.0,
+                scalar2=0.0,
+                op0=ALU.mult,
+                op1=ALU.add,
+            )
+            h_codes = work.tile([P, UNIT], U32, align_bytes=64)
+            h_scales = work.tile([P, UNIT], U8, align_bytes=64)
+            nc.vector.quantize_mx(
+                out=h_codes[:].bitcast(FP8X4),
+                scales=h_scales[:],
+                in_=h_grouped[:].rearrange("p n t -> p (n t)"),
+            )
+
+            biased = work.tile([P, UNIT_ROWS, MID], F32)
+            result = stores.tile([P, UNIT_ROWS, MID], F32)
+            for j in range(UNIT_ROWS):
+                j_cols = slice(j * P, (j + 1) * P)
+                out_ps = ps_out.tile([P, MID], F32)
+                nc.tensor.matmul_mx(
+                    out=out_ps[:],
+                    lhsT=h_codes[:, j_cols].bitcast(FP8X4),
+                    lhsT_scale=h_scales[:, j_cols],
+                    rhs=w1_codes[:].bitcast(FP8X4),
+                    rhs_scale=w1_scales[:],
+                    start=True,
+                    stop=True,
+                )
+                nc.vector.tensor_tensor(out=biased[:, j, :], in0=out_ps[:], in1=b1_all[:], op=ALU.add)
+                nc.scalar.activation(out=result[:, j, :], in_=biased[:, j, :], func=ACT.Gelu_apprx_tanh)
+            nc.sync.dma_start(out=out_rows[:, row0 : row0 + UNIT_ROWS, :], in_=result[:])

@@ -161,14 +161,7 @@ def tile_samplequerymessagepassing_pa_t_kernel(
                     out=h_planes[:, m, :], in_=h_ps[:], func=ACT.Gelu_apprx_tanh, bias=b0_cols[:, m : m + 1], scale=1.0
                 )
             h_grouped = work.tile([P, UNIT, PACK], BF16, align_bytes=64)
-            nc.gpsimd.tensor_scalar(
-                out=h_grouped[:],
-                in0=h_planes[:].rearrange("p t n -> p n t"),
-                scalar1=1.0,
-                scalar2=0.0,
-                op0=ALU.mult,
-                op1=ALU.add,
-            )
+            nc.vector.tensor_copy(out=h_grouped[:], in_=h_planes[:].rearrange("p t n -> p n t"))
             h_codes = work.tile([P, UNIT], U32, align_bytes=64)
             h_scales = work.tile([P, UNIT], U8, align_bytes=64)
             nc.vector.quantize_mx(

@@ -23,6 +23,9 @@ UNITS = ROWS // UNIT_ROWS
 CHUNK_ROWS = 8
 HALF = UNIT // 2
 SAMPLE_BUFS = 2
+TILES = TOKENS // P
+H_BANKS = 2
+OUT_BANKS = 3
 
 FLOPS = 2 * TOKENS * (2 * C * MID + MID * MID)
 
@@ -61,8 +64,8 @@ def tile_samplequerymessagepassing_pa_t_kernel(
         stores = ctx.enter_context(tc.tile_pool(name="stores", bufs=3))
         ps_sample = ctx.enter_context(tc.psum_pool(name="ps_sample", bufs=1))
         ps_q = ctx.enter_context(tc.psum_pool(name="ps_q", bufs=2))
-        ps_h = ctx.enter_context(tc.psum_pool(name="ps_h", bufs=3))
-        ps_out = ctx.enter_context(tc.psum_pool(name="ps_out", bufs=2))
+        ps_h = ctx.enter_context(tc.psum_pool(name="ps_h", bufs=H_BANKS))
+        ps_out = ctx.enter_context(tc.psum_pool(name="ps_out", bufs=OUT_BANKS))
 
         ident = keep.tile([P, P], BF16)
         make_identity(nc, ident[:])
@@ -92,98 +95,166 @@ def tile_samplequerymessagepassing_pa_t_kernel(
         b1_all = keep.tile([P, MID], F32)
         nc.vector.tensor_copy(out=b1_all[:], in_=b1_bf16[:])
 
-        chunk = {}
-        for unit in range(UNITS):
-            row0 = unit * UNIT_ROWS
-            if row0 % CHUNK_ROWS == 0:
-                cols = slice(row0 * C, (row0 + CHUNK_ROWS) * C)
-                query_pos = loads.tile([P, 2, CHUNK_ROWS * C], BF16)
-                nc.sync.dma_start(out=query_pos[0:P:2, :, :], in_=query_rows[:, :, cols])
-                nc.sync.dma_start(out=query_pos[1:P:2, :, :], in_=pos_rows[:, :, cols])
-                sample_sb = loads.tile([P, CHUNK_ROWS * C], BF16)
-                nc.sync.dma_start(out=sample_sb[:], in_=sample_rows[:, cols])
-                chunk = {"query_pos": query_pos, "sample": sample_sb}
+        live = {}
 
+        def is_unit(unit):
+            return 0 <= unit < UNITS
+
+        def load_chunk(index):
+            cols = slice(index * CHUNK_ROWS * C, (index + 1) * CHUNK_ROWS * C)
+            query_pos = loads.tile([P, 2, CHUNK_ROWS * C], BF16)
+            nc.sync.dma_start(out=query_pos[0:P:2, :, :], in_=query_rows[:, :, cols])
+            nc.sync.dma_start(out=query_pos[1:P:2, :, :], in_=pos_rows[:, :, cols])
+            sample_sb = loads.tile([P, CHUNK_ROWS * C], BF16)
+            nc.sync.dma_start(out=sample_sb[:], in_=sample_rows[:, cols])
+            live["query_pos", index] = query_pos
+            live["sample", index] = sample_sb
+
+        def channels(unit, j, c):
+            row = unit * UNIT_ROWS + j
+            first = (row % CHUNK_ROWS) * C + c * P
+            return row // CHUNK_ROWS, slice(first, first + P)
+
+        def turn_sample(unit):
             sample_ps = ps_sample.tile([P, 2, UNIT], BF16, tag="sample_ps")
-            q_banks = []
-            for half in range(2):
-                q_ps = ps_q.tile([P, 2, HALF], F32)
-                q_banks.append(q_ps)
             for j in range(UNIT_ROWS):
                 for c in range(2):
-                    first = ((row0 % CHUNK_ROWS) + j) * C + c * P
-                    nc.tensor.transpose(
-                        sample_ps[:, c, j * P : (j + 1) * P], chunk["sample"][:, first : first + P], ident[:]
-                    )
+                    index, cols = channels(unit, j, c)
+                    nc.tensor.transpose(sample_ps[:, c, j * P : (j + 1) * P], live["sample", index][:, cols], ident[:])
+            nc.scalar.copy(out=sample_t[unit % SAMPLE_BUFS][:, 0, :, :], in_=sample_ps[:])
+
+        def turn_query(unit, half):
+            q_ps = ps_q.tile([P, 2, HALF], F32)
+            for jj in range(2):
+                for c in range(2):
+                    index, cols = channels(unit, 2 * half + jj, c)
                     for a in range(2):
-                        n0 = (j % 2) * P + a * (P // 2)
+                        n0 = jj * P + a * (P // 2)
                         nc.tensor.matmul(
-                            out=q_banks[j // 2][:, c, n0 : n0 + P // 2],
-                            lhsT=chunk["query_pos"][:, a, first : first + P],
+                            out=q_ps[:, c, n0 : n0 + P // 2],
+                            lhsT=live["query_pos", index][:, a, cols],
                             rhs=add_pairs[:],
                             start=True,
                             stop=True,
                         )
-            sample_zero = sample_t[unit % SAMPLE_BUFS]
-            nc.scalar.copy(out=sample_zero[:, 0, :, :], in_=sample_ps[:])
+            live["q_ps", unit, half] = q_ps
 
-            x_grouped = work.tile([P, UNIT, PACK], BF16, align_bytes=64)
+        def make_x(unit, half):
+            if half == 0:
+                x_grouped = work.tile([P, UNIT, PACK], BF16, align_bytes=64)
+                live["x_grouped", unit] = x_grouped
+            tokens = slice(half * HALF, (half + 1) * HALF)
+            nc.vector.tensor_tensor(
+                out=live["x_grouped", unit][:, tokens, :].rearrange("p n (u c) -> p n u c", c=2),
+                in0=sample_t[unit % SAMPLE_BUFS][:, :, :, tokens].rearrange("p u c n -> p n u c"),
+                in1=live["q_ps", unit, half][:].rearrange("p c n -> p n c").unsqueeze(2).to_broadcast([P, HALF, 2, 2]),
+                op=ALU.subtract,
+            )
+
+        def quantise(grouped, name, unit):
+            codes = work.tile([P, UNIT], U32, name=name + "_codes", align_bytes=64)
+            scales = work.tile([P, UNIT], U8, name=name + "_scales", align_bytes=64)
             for half in range(2):
                 tokens = slice(half * HALF, (half + 1) * HALF)
-                nc.vector.tensor_tensor(
-                    out=x_grouped[:, tokens, :].rearrange("p n (u c) -> p n u c", c=2),
-                    in0=sample_zero[:, :, :, tokens].rearrange("p u c n -> p n u c"),
-                    in1=q_banks[half][:].rearrange("p c n -> p n c").unsqueeze(2).to_broadcast([P, HALF, 2, 2]),
-                    op=ALU.subtract,
+                nc.vector.quantize_mx(
+                    out=codes[:, tokens].bitcast(FP8X4),
+                    scales=scales[:, tokens],
+                    in_=grouped[:, tokens, :].rearrange("p n t -> p (n t)"),
                 )
-            x_codes = work.tile([P, UNIT], U32, align_bytes=64)
-            x_scales = work.tile([P, UNIT], U8, align_bytes=64)
-            nc.vector.quantize_mx(
-                out=x_codes[:].bitcast(FP8X4),
-                scales=x_scales[:],
-                in_=x_grouped[:].rearrange("p n t -> p (n t)"),
+            live[name + "_codes", unit] = codes
+            live[name + "_scales", unit] = scales
+
+        def layer1(unit, m):
+            if m == 0:
+                h_planes = work.tile([P, PACK, UNIT], BF16)
+                live["h_planes", unit] = h_planes
+            m_cols = slice(m * P, (m + 1) * P)
+            h_ps = ps_h.tile([P, UNIT], F32)
+            nc.tensor.matmul_mx(
+                out=h_ps[:],
+                lhsT=w0_codes[:, m_cols].bitcast(FP8X4),
+                lhsT_scale=w0_scales[:, m_cols],
+                rhs=live["x_codes", unit][:].bitcast(FP8X4),
+                rhs_scale=live["x_scales", unit][:],
+                start=True,
+                stop=True,
+            )
+            nc.scalar.activation(
+                out=live["h_planes", unit][:, m, :],
+                in_=h_ps[:],
+                func=ACT.Gelu_apprx_tanh,
+                bias=b0_cols[:, m : m + 1],
+                scale=1.0,
             )
 
-            h_planes = work.tile([P, PACK, UNIT], BF16)
-            for m in range(PACK):
-                m_cols = slice(m * P, (m + 1) * P)
-                h_ps = ps_h.tile([P, UNIT], F32)
-                nc.tensor.matmul_mx(
-                    out=h_ps[:],
-                    lhsT=w0_codes[:, m_cols].bitcast(FP8X4),
-                    lhsT_scale=w0_scales[:, m_cols],
-                    rhs=x_codes[:].bitcast(FP8X4),
-                    rhs_scale=x_scales[:],
-                    start=True,
-                    stop=True,
-                )
-                nc.scalar.activation(
-                    out=h_planes[:, m, :], in_=h_ps[:], func=ACT.Gelu_apprx_tanh, bias=b0_cols[:, m : m + 1], scale=1.0
-                )
+        def regroup_h(unit):
             h_grouped = work.tile([P, UNIT, PACK], BF16, align_bytes=64)
-            nc.vector.tensor_copy(out=h_grouped[:], in_=h_planes[:].rearrange("p t n -> p n t"))
-            h_codes = work.tile([P, UNIT], U32, align_bytes=64)
-            h_scales = work.tile([P, UNIT], U8, align_bytes=64)
-            nc.vector.quantize_mx(
-                out=h_codes[:].bitcast(FP8X4),
-                scales=h_scales[:],
-                in_=h_grouped[:].rearrange("p n t -> p (n t)"),
+            nc.gpsimd.tensor_scalar(
+                out=h_grouped[:],
+                in0=live["h_planes", unit][:].rearrange("p t n -> p n t"),
+                scalar1=1.0,
+                scalar2=0.0,
+                op0=ALU.mult,
+                op1=ALU.add,
+            )
+            live["h_grouped", unit] = h_grouped
+
+        def layer2(row_tile):
+            unit, j = divmod(row_tile, UNIT_ROWS)
+            j_cols = slice(j * P, (j + 1) * P)
+            out_ps = ps_out.tile([P, MID], F32)
+            nc.tensor.matmul_mx(
+                out=out_ps[:],
+                lhsT=live["h_codes", unit][:, j_cols].bitcast(FP8X4),
+                lhsT_scale=live["h_scales", unit][:, j_cols],
+                rhs=w1_codes[:].bitcast(FP8X4),
+                rhs_scale=w1_scales[:],
+                start=True,
+                stop=True,
+            )
+            live["out_ps", row_tile] = out_ps
+
+        def add_b1(row_tile):
+            unit, j = divmod(row_tile, UNIT_ROWS)
+            if j == 0:
+                biased = work.tile([P, UNIT_ROWS, MID], F32)
+                live["biased", unit] = biased
+            nc.vector.tensor_tensor(
+                out=live["biased", unit][:, j, :], in0=live["out_ps", row_tile][:], in1=b1_all[:], op=ALU.add
             )
 
-            biased = work.tile([P, UNIT_ROWS, MID], F32)
+        def finish(unit):
             result = stores.tile([P, UNIT_ROWS, MID], F32)
-            for j in range(UNIT_ROWS):
-                j_cols = slice(j * P, (j + 1) * P)
-                out_ps = ps_out.tile([P, MID], F32)
-                nc.tensor.matmul_mx(
-                    out=out_ps[:],
-                    lhsT=h_codes[:, j_cols].bitcast(FP8X4),
-                    lhsT_scale=h_scales[:, j_cols],
-                    rhs=w1_codes[:].bitcast(FP8X4),
-                    rhs_scale=w1_scales[:],
-                    start=True,
-                    stop=True,
-                )
-                nc.vector.tensor_tensor(out=biased[:, j, :], in0=out_ps[:], in1=b1_all[:], op=ALU.add)
-                nc.scalar.activation(out=result[:, j, :], in_=biased[:, j, :], func=ACT.Gelu_apprx_tanh)
+            nc.scalar.activation(out=result[:], in_=live["biased", unit][:], func=ACT.Gelu_apprx_tanh)
+            row0 = unit * UNIT_ROWS
             nc.sync.dma_start(out=out_rows[:, row0 : row0 + UNIT_ROWS, :], in_=result[:])
+
+        load_chunk(0)
+        load_chunk(1)
+        with tc.manual_schedule():
+            for step in range(-1, UNITS + 4):
+                for j in range(UNIT_ROWS):
+                    if is_unit(step - 1):
+                        layer1(step - 1, j)
+                    row_tile = (step - 4) * UNIT_ROWS + j
+                    if 0 <= row_tile:
+                        add_b1(row_tile)
+                    if 0 <= row_tile + OUT_BANKS < TILES:
+                        layer2(row_tile + OUT_BANKS)
+                if is_unit(step - 4):
+                    finish(step - 4)
+                if is_unit(step - 1):
+                    regroup_h(step - 1)
+                if is_unit(step - 2):
+                    quantise(live["h_grouped", step - 2], "h", step - 2)
+                if is_unit(step + 1):
+                    turn_sample(step + 1)
+                for half in range(2):
+                    if is_unit(step):
+                        make_x(step, half)
+                    if is_unit(step + 1):
+                        turn_query(step + 1, half)
+                if is_unit(step):
+                    quantise(live["x_grouped", step], "x", step)
+                if is_unit(step + 4) and (step + 4) * UNIT_ROWS % CHUNK_ROWS == 0:
+                    load_chunk((step + 4) * UNIT_ROWS // CHUNK_ROWS)

@@ -20,19 +20,16 @@ ROWS = TOKENS // P
 UNIT_ROWS = 4
 UNIT = UNIT_ROWS * P
 UNITS = ROWS // UNIT_ROWS
-CHUNK_ROWS = 8
 HALF = UNIT // 2
 SAMPLE_BUFS = 2
-TILES = TOKENS // P
 H_BANKS = 2
 OUT_BANKS = 3
+PREFETCH = 4
 
 FLOPS = 2 * TOKENS * (2 * C * MID + MID * MID)
 
 
-def quantise_weight(nc, stage, keep, weight, negated, name):
-    raw = stage.tile([P, PACK, MID], BF16, name=name + "_raw")
-    nc.sync.dma_start(out=raw[:], in_=weight.rearrange("(t p) n -> p t n", p=P))
+def quantise_weight(nc, stage, keep, raw, negated, name):
     if negated:
         nc.vector.tensor_scalar_mul(out=raw[:, PACK - negated :, :], in0=raw[:, PACK - negated :, :], scalar1=-1.0)
     grouped = stage.tile([P, MID, PACK], BF16, name=name + "_grouped", align_bytes=64)
@@ -59,13 +56,41 @@ def tile_samplequerymessagepassing_pa_t_kernel(
     with ExitStack() as ctx:
         keep = ctx.enter_context(tc.tile_pool(name="keep", bufs=1))
         stage = ctx.enter_context(tc.tile_pool(name="stage", bufs=1))
-        loads = ctx.enter_context(tc.tile_pool(name="loads", bufs=3))
+        loads = ctx.enter_context(tc.tile_pool(name="loads", bufs=PREFETCH))
         work = ctx.enter_context(tc.tile_pool(name="work", bufs=2))
         stores = ctx.enter_context(tc.tile_pool(name="stores", bufs=3))
         ps_sample = ctx.enter_context(tc.psum_pool(name="ps_sample", bufs=1))
         ps_q = ctx.enter_context(tc.psum_pool(name="ps_q", bufs=2))
         ps_h = ctx.enter_context(tc.psum_pool(name="ps_h", bufs=H_BANKS))
         ps_out = ctx.enter_context(tc.psum_pool(name="ps_out", bufs=OUT_BANKS))
+
+        live = {}
+
+        def is_unit(unit):
+            return 0 <= unit < UNITS
+
+        def load_unit(unit):
+            cols = slice(unit * UNIT_ROWS * C, (unit + 1) * UNIT_ROWS * C)
+            query_pos = loads.tile([P, 2, UNIT_ROWS * C], BF16)
+            nc.sync.dma_start(out=query_pos[0:P:2, :, :], in_=query_rows[:, :, cols])
+            nc.sync.dma_start(out=query_pos[1:P:2, :, :], in_=pos_rows[:, :, cols])
+            sample_sb = loads.tile([P, UNIT_ROWS * C], BF16)
+            nc.sync.dma_start(out=sample_sb[:], in_=sample_rows[:, cols])
+            live["query_pos", unit] = query_pos
+            live["sample", unit] = sample_sb
+
+        w0_raw = stage.tile([P, PACK, MID], BF16)
+        nc.scalar.dma_start(out=w0_raw[:], in_=W0.rearrange("(t p) n -> p t n", p=P))
+        b0_rows = stage.tile([P, P], BF16)
+        nc.vector.memset(b0_rows[:], 0.0)
+        nc.scalar.dma_start(out=b0_rows[0:PACK, :], in_=b0.rearrange("(m p) -> m p", p=P))
+        load_unit(0)
+        load_unit(1)
+        w1_raw = stage.tile([P, PACK, MID], BF16)
+        nc.sync.dma_start(out=w1_raw[:], in_=W1.rearrange("(t p) n -> p t n", p=P))
+        b1_bf16 = stage.tile([P, MID], BF16)
+        nc.sync.dma_start(out=b1_bf16[:], in_=b1.partition_broadcast(P))
+        load_unit(2)
 
         ident = keep.tile([P, P], BF16)
         make_identity(nc, ident[:])
@@ -79,60 +104,35 @@ def tile_samplequerymessagepassing_pa_t_kernel(
             nc.vector.memset(sample_zero[:, 1, :, :], 0.0)
             sample_t.append(sample_zero)
 
-        w0_codes, w0_scales = quantise_weight(nc, stage, keep, W0, 2, "w0")
-        w1_codes, w1_scales = quantise_weight(nc, stage, keep, W1, 0, "w1")
+        w0_codes, w0_scales = quantise_weight(nc, stage, keep, w0_raw, 2, "w0")
 
-        b0_rows = stage.tile([P, P], BF16)
-        nc.vector.memset(b0_rows[:], 0.0)
-        nc.sync.dma_start(out=b0_rows[0:PACK, :], in_=b0.rearrange("(m p) -> m p", p=P))
         b0_ps = ps_sample.tile([P, P], BF16, tag="sample_ps")
         nc.tensor.transpose(b0_ps[:], b0_rows[:], ident[:])
         b0_cols = keep.tile([P, PACK], F32)
         nc.vector.tensor_copy(out=b0_cols[:], in_=b0_ps[:, 0:PACK])
 
-        b1_bf16 = stage.tile([P, MID], BF16)
-        nc.sync.dma_start(out=b1_bf16[:], in_=b1.partition_broadcast(P))
+        grouped = keep.tile([P, 2, UNIT, PACK], BF16, align_bytes=64)
         b1_all = keep.tile([P, MID], F32)
-        nc.vector.tensor_copy(out=b1_all[:], in_=b1_bf16[:])
 
-        live = {}
-
-        def is_unit(unit):
-            return 0 <= unit < UNITS
-
-        def load_chunk(index):
-            cols = slice(index * CHUNK_ROWS * C, (index + 1) * CHUNK_ROWS * C)
-            query_pos = loads.tile([P, 2, CHUNK_ROWS * C], BF16)
-            nc.sync.dma_start(out=query_pos[0:P:2, :, :], in_=query_rows[:, :, cols])
-            nc.sync.dma_start(out=query_pos[1:P:2, :, :], in_=pos_rows[:, :, cols])
-            sample_sb = loads.tile([P, CHUNK_ROWS * C], BF16)
-            nc.sync.dma_start(out=sample_sb[:], in_=sample_rows[:, cols])
-            live["query_pos", index] = query_pos
-            live["sample", index] = sample_sb
-
-        def channels(unit, j, c):
-            row = unit * UNIT_ROWS + j
-            first = (row % CHUNK_ROWS) * C + c * P
-            return row // CHUNK_ROWS, slice(first, first + P)
+        def channels(j, c):
+            return slice(j * C + c * P, j * C + (c + 1) * P)
 
         def turn_sample(unit):
             sample_ps = ps_sample.tile([P, 2, UNIT], BF16, tag="sample_ps")
             for j in range(UNIT_ROWS):
                 for c in range(2):
-                    index, cols = channels(unit, j, c)
-                    nc.tensor.transpose(sample_ps[:, c, j * P : (j + 1) * P], live["sample", index][:, cols], ident[:])
+                    nc.tensor.transpose(sample_ps[:, c, j * P : (j + 1) * P], live["sample", unit][:, channels(j, c)], ident[:])
             nc.scalar.copy(out=sample_t[unit % SAMPLE_BUFS][:, 0, :, :], in_=sample_ps[:])
 
         def turn_query(unit, half):
             q_ps = ps_q.tile([P, 2, HALF], F32)
             for jj in range(2):
                 for c in range(2):
-                    index, cols = channels(unit, 2 * half + jj, c)
                     for a in range(2):
                         n0 = jj * P + a * (P // 2)
                         nc.tensor.matmul(
                             out=q_ps[:, c, n0 : n0 + P // 2],
-                            lhsT=live["query_pos", index][:, a, cols],
+                            lhsT=live["query_pos", unit][:, a, channels(2 * half + jj, c)],
                             rhs=add_pairs[:],
                             start=True,
                             stop=True,
@@ -140,42 +140,40 @@ def tile_samplequerymessagepassing_pa_t_kernel(
             live["q_ps", unit, half] = q_ps
 
         def make_x(unit, half):
-            if half == 0:
-                x_grouped = work.tile([P, UNIT, PACK], BF16, align_bytes=64)
-                live["x_grouped", unit] = x_grouped
             tokens = slice(half * HALF, (half + 1) * HALF)
             nc.vector.tensor_tensor(
-                out=live["x_grouped", unit][:, tokens, :].rearrange("p n (u c) -> p n u c", c=2),
+                out=grouped[:, 0, tokens, :].rearrange("p n (u c) -> p n u c", c=2),
                 in0=sample_t[unit % SAMPLE_BUFS][:, :, :, tokens].rearrange("p u c n -> p n u c"),
                 in1=live["q_ps", unit, half][:].rearrange("p c n -> p n c").unsqueeze(2).to_broadcast([P, HALF, 2, 2]),
                 op=ALU.subtract,
             )
 
-        def quantise(grouped, name, unit):
-            codes = work.tile([P, UNIT], U32, name=name + "_codes", align_bytes=64)
-            scales = work.tile([P, UNIT], U8, name=name + "_scales", align_bytes=64)
-            for half in range(2):
-                tokens = slice(half * HALF, (half + 1) * HALF)
-                nc.vector.quantize_mx(
-                    out=codes[:, tokens].bitcast(FP8X4),
-                    scales=scales[:, tokens],
-                    in_=grouped[:, tokens, :].rearrange("p n t -> p (n t)"),
-                )
-            live[name + "_codes", unit] = codes
-            live[name + "_scales", unit] = scales
+        def quantise(x_unit, h_unit):
+            first = 0 if is_unit(x_unit) else 1
+            last = 2 if is_unit(h_unit) else 1
+            codes = work.tile([P, 2, UNIT], U32, align_bytes=64)
+            scales = work.tile([P, 2, UNIT], U8, align_bytes=64)
+            nc.vector.quantize_mx(
+                out=codes[:, first:last, :].rearrange("p g n -> p (g n)").bitcast(FP8X4),
+                scales=scales[:, first:last, :].rearrange("p g n -> p (g n)"),
+                in_=grouped[:, first:last, :, :].rearrange("p g n t -> p (g n t)"),
+            )
+            live["x", x_unit] = (codes[:, 0, :], scales[:, 0, :])
+            live["h", h_unit] = (codes[:, 1, :], scales[:, 1, :])
 
         def layer1(unit, m):
             if m == 0:
                 h_planes = work.tile([P, PACK, UNIT], BF16)
                 live["h_planes", unit] = h_planes
+            x_codes, x_scales = live["x", unit]
             m_cols = slice(m * P, (m + 1) * P)
             h_ps = ps_h.tile([P, UNIT], F32)
             nc.tensor.matmul_mx(
                 out=h_ps[:],
                 lhsT=w0_codes[:, m_cols].bitcast(FP8X4),
                 lhsT_scale=w0_scales[:, m_cols],
-                rhs=live["x_codes", unit][:].bitcast(FP8X4),
-                rhs_scale=live["x_scales", unit][:],
+                rhs=x_codes.bitcast(FP8X4),
+                rhs_scale=x_scales,
                 start=True,
                 stop=True,
             )
@@ -188,65 +186,47 @@ def tile_samplequerymessagepassing_pa_t_kernel(
             )
 
         def regroup_h(unit):
-            h_grouped = work.tile([P, UNIT, PACK], BF16, align_bytes=64)
             nc.gpsimd.tensor_scalar(
-                out=h_grouped[:],
+                out=grouped[:, 1, :, :],
                 in0=live["h_planes", unit][:].rearrange("p t n -> p n t"),
                 scalar1=1.0,
                 scalar2=0.0,
                 op0=ALU.mult,
                 op1=ALU.add,
             )
-            live["h_grouped", unit] = h_grouped
 
-        def layer2(row_tile):
-            unit, j = divmod(row_tile, UNIT_ROWS)
+        def layer2(unit, j):
+            h_codes, h_scales = live["h", unit]
+            w1_codes, w1_scales = live["w1"]
             j_cols = slice(j * P, (j + 1) * P)
             out_ps = ps_out.tile([P, MID], F32)
             nc.tensor.matmul_mx(
                 out=out_ps[:],
-                lhsT=live["h_codes", unit][:, j_cols].bitcast(FP8X4),
-                lhsT_scale=live["h_scales", unit][:, j_cols],
+                lhsT=h_codes[:, j_cols].bitcast(FP8X4),
+                lhsT_scale=h_scales[:, j_cols],
                 rhs=w1_codes[:].bitcast(FP8X4),
                 rhs_scale=w1_scales[:],
                 start=True,
                 stop=True,
             )
-            live["out_ps", row_tile] = out_ps
+            live["out_ps", unit, j] = out_ps
 
-        def add_b1(row_tile):
-            unit, j = divmod(row_tile, UNIT_ROWS)
+        def add_b1(unit, j):
             if j == 0:
                 biased = work.tile([P, UNIT_ROWS, MID], F32)
                 live["biased", unit] = biased
             nc.vector.tensor_tensor(
-                out=live["biased", unit][:, j, :], in0=live["out_ps", row_tile][:], in1=b1_all[:], op=ALU.add
+                out=live["biased", unit][:, j, :], in0=live["out_ps", unit, j][:], in1=b1_all[:], op=ALU.add
             )
 
-        def finish(unit):
-            result = stores.tile([P, UNIT_ROWS, MID], F32)
-            nc.scalar.activation(out=result[:], in_=live["biased", unit][:], func=ACT.Gelu_apprx_tanh)
-            row0 = unit * UNIT_ROWS
-            nc.sync.dma_start(out=out_rows[:, row0 : row0 + UNIT_ROWS, :], in_=result[:])
+        def finish(unit, j0):
+            result = stores.tile([P, 2, MID], F32)
+            nc.scalar.activation(out=result[:], in_=live["biased", unit][:, j0 : j0 + 2, :], func=ACT.Gelu_apprx_tanh)
+            row0 = unit * UNIT_ROWS + j0
+            nc.sync.dma_start(out=out_rows[:, row0 : row0 + 2, :], in_=result[:])
 
-        load_chunk(0)
-        load_chunk(1)
         with tc.manual_schedule():
-            for step in range(-1, UNITS + 4):
-                for j in range(UNIT_ROWS):
-                    if is_unit(step - 1):
-                        layer1(step - 1, j)
-                    row_tile = (step - 4) * UNIT_ROWS + j
-                    if 0 <= row_tile:
-                        add_b1(row_tile)
-                    if 0 <= row_tile + OUT_BANKS < TILES:
-                        layer2(row_tile + OUT_BANKS)
-                if is_unit(step - 4):
-                    finish(step - 4)
-                if is_unit(step - 1):
-                    regroup_h(step - 1)
-                if is_unit(step - 2):
-                    quantise(live["h_grouped", step - 2], "h", step - 2)
+            for step in range(-1, UNITS + 3):
                 if is_unit(step + 1):
                     turn_sample(step + 1)
                 for half in range(2):
@@ -254,7 +234,25 @@ def tile_samplequerymessagepassing_pa_t_kernel(
                         make_x(step, half)
                     if is_unit(step + 1):
                         turn_query(step + 1, half)
-                if is_unit(step):
-                    quantise(live["x_grouped", step], "x", step)
-                if is_unit(step + 4) and (step + 4) * UNIT_ROWS % CHUNK_ROWS == 0:
-                    load_chunk((step + 4) * UNIT_ROWS // CHUNK_ROWS)
+                if is_unit(step - 3):
+                    for j in range(UNIT_ROWS):
+                        add_b1(step - 3, j)
+                        if j + OUT_BANKS < UNIT_ROWS:
+                            layer2(step - 3, j + OUT_BANKS)
+                        if j % 2 == 1:
+                            finish(step - 3, j - 1)
+                if is_unit(step) or is_unit(step - 2):
+                    quantise(step, step - 2)
+                if is_unit(step - 1):
+                    regroup_h(step - 1)
+                if step == 0:
+                    live["w1"] = quantise_weight(nc, stage, keep, w1_raw, 0, "w1")
+                    nc.vector.tensor_copy(out=b1_all[:], in_=b1_bf16[:])
+                for m in range(PACK):
+                    if m == H_BANKS and is_unit(step - 2):
+                        for j in range(OUT_BANKS):
+                            layer2(step - 2, j)
+                    if is_unit(step):
+                        layer1(step, m)
+                if is_unit(step + PREFETCH):
+                    load_unit(step + PREFETCH)

@@ -88,8 +88,8 @@ def tile_samplequerymessagepassing_pa_t_kernel(
         load_unit(1)
         w1_raw = stage.tile([P, PACK, MID], BF16)
         nc.sync.dma_start(out=w1_raw[:], in_=W1.rearrange("(t p) n -> p t n", p=P))
-        b1_bf16 = stage.tile([P, MID], BF16)
-        nc.sync.dma_start(out=b1_bf16[:], in_=b1.partition_broadcast(P))
+        b1_all = keep.tile([P, MID], BF16)
+        nc.sync.dma_start(out=b1_all[:], in_=b1.partition_broadcast(P))
         load_unit(2)
 
         ident = keep.tile([P, P], BF16)
@@ -100,7 +100,7 @@ def tile_samplequerymessagepassing_pa_t_kernel(
 
         sample_t = []
         for i in range(SAMPLE_BUFS):
-            sample_zero = keep.tile([P, 2, 2, UNIT], BF16, name="sample_zero%d" % i)
+            sample_zero = keep.tile([P, 2, UNIT, 2], BF16, name="sample_zero%d" % i)
             nc.vector.memset(sample_zero[:, 1, :, :], 0.0)
             sample_t.append(sample_zero)
 
@@ -112,7 +112,6 @@ def tile_samplequerymessagepassing_pa_t_kernel(
         nc.vector.tensor_copy(out=b0_cols[:], in_=b0_ps[:, 0:PACK])
 
         grouped = keep.tile([P, 2, UNIT, PACK], BF16, align_bytes=64)
-        b1_all = keep.tile([P, MID], F32)
 
         def channels(j, c):
             return slice(j * C + c * P, j * C + (c + 1) * P)
@@ -122,7 +121,7 @@ def tile_samplequerymessagepassing_pa_t_kernel(
             for j in range(UNIT_ROWS):
                 for c in range(2):
                     nc.tensor.transpose(sample_ps[:, c, j * P : (j + 1) * P], live["sample", unit][:, channels(j, c)], ident[:])
-            nc.scalar.copy(out=sample_t[unit % SAMPLE_BUFS][:, 0, :, :], in_=sample_ps[:])
+            nc.scalar.copy(out=sample_t[unit % SAMPLE_BUFS][:, 0, :, :], in_=sample_ps[:].rearrange("p c n -> p n c"))
 
         def turn_query(unit, half):
             q_ps = ps_q.tile([P, 2, HALF], F32)
@@ -143,7 +142,7 @@ def tile_samplequerymessagepassing_pa_t_kernel(
             tokens = slice(half * HALF, (half + 1) * HALF)
             nc.vector.tensor_tensor(
                 out=grouped[:, 0, tokens, :].rearrange("p n (u c) -> p n u c", c=2),
-                in0=sample_t[unit % SAMPLE_BUFS][:, :, :, tokens].rearrange("p u c n -> p n u c"),
+                in0=sample_t[unit % SAMPLE_BUFS][:, :, tokens, :].rearrange("p u n c -> p n u c"),
                 in1=live["q_ps", unit, half][:].rearrange("p c n -> p n c").unsqueeze(2).to_broadcast([P, HALF, 2, 2]),
                 op=ALU.subtract,
             )
@@ -247,7 +246,6 @@ def tile_samplequerymessagepassing_pa_t_kernel(
                     regroup_h(step - 1)
                 if step == 0:
                     live["w1"] = quantise_weight(nc, stage, keep, w1_raw, 0, "w1")
-                    nc.vector.tensor_copy(out=b1_all[:], in_=b1_bf16[:])
                 for m in range(PACK):
                     if m == H_BANKS and is_unit(step - 2):
                         for j in range(OUT_BANKS):

@@ -25,6 +25,7 @@ SAMPLE_BUFS = 2
 H_BANKS = 2
 OUT_BANKS = 3
 PREFETCH = 4
+VECTOR_ROWS = 3
 
 FLOPS = 2 * TOKENS * (2 * C * MID + MID * MID)
 
@@ -88,8 +89,8 @@ def tile_samplequerymessagepassing_pa_t_kernel(
         load_unit(1)
         w1_raw = stage.tile([P, PACK, MID], BF16)
         nc.sync.dma_start(out=w1_raw[:], in_=W1.rearrange("(t p) n -> p t n", p=P))
-        b1_all = keep.tile([P, MID], BF16)
-        nc.sync.dma_start(out=b1_all[:], in_=b1.partition_broadcast(P))
+        b1_bf16 = stage.tile([P, MID], BF16)
+        nc.sync.dma_start(out=b1_bf16[:], in_=b1.partition_broadcast(P))
         load_unit(2)
 
         ident = keep.tile([P, P], BF16)
@@ -100,7 +101,7 @@ def tile_samplequerymessagepassing_pa_t_kernel(
 
         sample_t = []
         for i in range(SAMPLE_BUFS):
-            sample_zero = keep.tile([P, 2, UNIT, 2], BF16, name="sample_zero%d" % i)
+            sample_zero = keep.tile([P, 2, 2, UNIT], BF16, name="sample_zero%d" % i)
             nc.vector.memset(sample_zero[:, 1, :, :], 0.0)
             sample_t.append(sample_zero)
 
@@ -112,6 +113,7 @@ def tile_samplequerymessagepassing_pa_t_kernel(
         nc.vector.tensor_copy(out=b0_cols[:], in_=b0_ps[:, 0:PACK])
 
         grouped = keep.tile([P, 2, UNIT, PACK], BF16, align_bytes=64)
+        b1_all = keep.tile([P, MID], F32)
 
         def channels(j, c):
             return slice(j * C + c * P, j * C + (c + 1) * P)
@@ -121,7 +123,7 @@ def tile_samplequerymessagepassing_pa_t_kernel(
             for j in range(UNIT_ROWS):
                 for c in range(2):
                     nc.tensor.transpose(sample_ps[:, c, j * P : (j + 1) * P], live["sample", unit][:, channels(j, c)], ident[:])
-            nc.scalar.copy(out=sample_t[unit % SAMPLE_BUFS][:, 0, :, :], in_=sample_ps[:].rearrange("p c n -> p n c"))
+            nc.scalar.copy(out=sample_t[unit % SAMPLE_BUFS][:, 0, :, :], in_=sample_ps[:])
 
         def turn_query(unit, half):
             q_ps = ps_q.tile([P, 2, HALF], F32)
@@ -142,7 +144,7 @@ def tile_samplequerymessagepassing_pa_t_kernel(
             tokens = slice(half * HALF, (half + 1) * HALF)
             nc.vector.tensor_tensor(
                 out=grouped[:, 0, tokens, :].rearrange("p n (u c) -> p n u c", c=2),
-                in0=sample_t[unit % SAMPLE_BUFS][:, :, tokens, :].rearrange("p u n c -> p n u c"),
+                in0=sample_t[unit % SAMPLE_BUFS][:, :, :, tokens].rearrange("p u c n -> p n u c"),
                 in1=live["q_ps", unit, half][:].rearrange("p c n -> p n c").unsqueeze(2).to_broadcast([P, HALF, 2, 2]),
                 op=ALU.subtract,
             )
@@ -184,10 +186,11 @@ def tile_samplequerymessagepassing_pa_t_kernel(
                 scale=1.0,
             )
 
-        def regroup_h(unit):
+        def regroup_h(unit, half):
+            tokens = slice(half * HALF, (half + 1) * HALF)
             nc.gpsimd.tensor_scalar(
-                out=grouped[:, 1, :, :],
-                in0=live["h_planes", unit][:].rearrange("p t n -> p n t"),
+                out=grouped[:, 1, tokens, :],
+                in0=live["h_planes", unit][:, :, tokens].rearrange("p t n -> p n t"),
                 scalar1=1.0,
                 scalar2=0.0,
                 op0=ALU.mult,
@@ -218,6 +221,14 @@ def tile_samplequerymessagepassing_pa_t_kernel(
                 out=live["biased", unit][:, j, :], in0=live["out_ps", unit, j][:], in1=b1_all[:], op=ALU.add
             )
 
+        def copy_last(unit):
+            j = UNIT_ROWS - 1
+            nc.scalar.copy(out=live["biased", unit][:, j, :], in_=live["out_ps", unit, j][:])
+
+        def add_b1_last(unit):
+            last = live["biased", unit][:, UNIT_ROWS - 1, :]
+            nc.gpsimd.tensor_tensor(out=last, in0=last, in1=b1_all[:], op=ALU.add)
+
         def finish(unit, j0):
             result = stores.tile([P, 2, MID], F32)
             nc.scalar.activation(out=result[:], in_=live["biased", unit][:, j0 : j0 + 2, :], func=ACT.Gelu_apprx_tanh)
@@ -225,7 +236,9 @@ def tile_samplequerymessagepassing_pa_t_kernel(
             nc.sync.dma_start(out=out_rows[:, row0 : row0 + 2, :], in_=result[:])
 
         with tc.manual_schedule():
-            for step in range(-1, UNITS + 3):
+            for step in range(-1, UNITS + 4):
+                if is_unit(step - 4):
+                    finish(step - 4, 2)
                 if is_unit(step + 1):
                     turn_sample(step + 1)
                 for half in range(2):
@@ -234,18 +247,24 @@ def tile_samplequerymessagepassing_pa_t_kernel(
                     if is_unit(step + 1):
                         turn_query(step + 1, half)
                 if is_unit(step - 3):
-                    for j in range(UNIT_ROWS):
+                    for j in range(VECTOR_ROWS):
                         add_b1(step - 3, j)
                         if j + OUT_BANKS < UNIT_ROWS:
                             layer2(step - 3, j + OUT_BANKS)
-                        if j % 2 == 1:
-                            finish(step - 3, j - 1)
+                        if j == 1:
+                            finish(step - 3, 0)
+                    copy_last(step - 3)
                 if is_unit(step) or is_unit(step - 2):
                     quantise(step, step - 2)
                 if is_unit(step - 1):
-                    regroup_h(step - 1)
+                    regroup_h(step - 1, 0)
+                if is_unit(step - 3):
+                    add_b1_last(step - 3)
+                if is_unit(step - 1):
+                    regroup_h(step - 1, 1)
                 if step == 0:
                     live["w1"] = quantise_weight(nc, stage, keep, w1_raw, 0, "w1")
+                    nc.vector.tensor_copy(out=b1_all[:], in_=b1_bf16[:])
                 for m in range(PACK):
                     if m == H_BANKS and is_unit(step - 2):
                         for j in range(OUT_BANKS):

@@ -20,48 +20,39 @@ ROWS = TOKENS // P
 UNIT_ROWS = 4
 UNIT = UNIT_ROWS * P
 UNITS = ROWS // UNIT_ROWS
-HALF = UNIT // 2
-SAMPLE_BUFS = 2
+WOVEN_ROWS = 3
+WOVEN = WOVEN_ROWS * UNITS
+STREAMS = 32
+WEAVE = 4
+SETS = P // STREAMS
 H_BANKS = 2
 OUT_BANKS = 3
-PREFETCH = 4
-VECTOR_ROWS = 3
+PLAIN_UNITS = 2
+WOVEN_BUFS = 3
+CHUNKS = [(0, 1), (1, 1)] + [(u, 2) for u in range(2, UNITS, 2)]
 
 FLOPS = 2 * TOKENS * (2 * C * MID + MID * MID)
-
-
-def quantise_weight(nc, stage, keep, raw, negated, name):
-    if negated:
-        nc.vector.tensor_scalar_mul(out=raw[:, PACK - negated :, :], in0=raw[:, PACK - negated :, :], scalar1=-1.0)
-    grouped = stage.tile([P, MID, PACK], BF16, name=name + "_grouped", align_bytes=64)
-    nc.vector.tensor_copy(out=grouped[:], in_=raw[:].rearrange("p t n -> p n t"))
-    codes = keep.tile([P, MID], U32, name=name + "_codes", align_bytes=64)
-    scales = keep.tile([P, MID], U8, name=name + "_scales", align_bytes=64)
-    nc.vector.quantize_mx(
-        out=codes[:].bitcast(FP8X4),
-        scales=scales[:],
-        in_=grouped[:].rearrange("p n t -> p (n t)"),
-    )
-    return codes, scales
 
 
 def tile_samplequerymessagepassing_pa_t_kernel(
     tc, sample_features, query_samples, pos_enc, W0, b0, W1, b1, out
 ):
     nc = tc.nc
-    sample_rows = sample_features.rearrange("b s c -> (b s) c").rearrange("(p r) c -> p (r c)", p=P)
+    inputs = (sample_features, query_samples, pos_enc)
+    woven_views = [
+        x.rearrange("b s c -> (b s) c").rearrange("(r n row) c -> n r (row c)", r=SETS, n=STREAMS) for x in inputs
+    ]
+    plain_views = [x.rearrange("b s c -> (b s) c").rearrange("(p row) c -> p (row c)", p=P) for x in inputs]
     out_rows = out.rearrange("b s m -> (b s) m").rearrange("(p r) m -> p r m", p=P)
-    query_rows = query_samples.rearrange("b s c -> (b s) c").rearrange("(a n r) c -> n a (r c)", a=2, r=ROWS)
-    pos_rows = pos_enc.rearrange("b s c -> (b s) c").rearrange("(a n r) c -> n a (r c)", a=2, r=ROWS)
 
     with ExitStack() as ctx:
+        ctx.enter_context(tc.manual_schedule())
         keep = ctx.enter_context(tc.tile_pool(name="keep", bufs=1))
         stage = ctx.enter_context(tc.tile_pool(name="stage", bufs=1))
-        loads = ctx.enter_context(tc.tile_pool(name="loads", bufs=PREFETCH))
+        loads = ctx.enter_context(tc.tile_pool(name="loads", bufs=3))
         work = ctx.enter_context(tc.tile_pool(name="work", bufs=2))
         stores = ctx.enter_context(tc.tile_pool(name="stores", bufs=3))
-        ps_sample = ctx.enter_context(tc.psum_pool(name="ps_sample", bufs=1))
-        ps_q = ctx.enter_context(tc.psum_pool(name="ps_q", bufs=2))
+        ps_x = ctx.enter_context(tc.psum_pool(name="ps_x", bufs=1))
         ps_h = ctx.enter_context(tc.psum_pool(name="ps_h", bufs=H_BANKS))
         ps_out = ctx.enter_context(tc.psum_pool(name="ps_out", bufs=OUT_BANKS))
 
@@ -70,82 +61,159 @@ def tile_samplequerymessagepassing_pa_t_kernel(
         def is_unit(unit):
             return 0 <= unit < UNITS
 
-        def load_unit(unit):
-            cols = slice(unit * UNIT_ROWS * C, (unit + 1) * UNIT_ROWS * C)
-            query_pos = loads.tile([P, 2, UNIT_ROWS * C], BF16)
-            nc.sync.dma_start(out=query_pos[0:P:2, :, :], in_=query_rows[:, :, cols])
-            nc.sync.dma_start(out=query_pos[1:P:2, :, :], in_=pos_rows[:, :, cols])
-            sample_sb = loads.tile([P, UNIT_ROWS * C], BF16)
-            nc.sync.dma_start(out=sample_sb[:], in_=sample_rows[:, cols])
-            live["query_pos", unit] = query_pos
-            live["sample", unit] = sample_sb
+        woven_bufs = []
+        for i in range(WOVEN_BUFS):
+            woven = keep.tile([P, SETS, 2 * WOVEN_ROWS * C], BF16, name="woven%d" % i)
+            woven_bufs.append(woven)
 
+        def load_woven(k):
+            first, count = CHUNKS[k]
+            woven = woven_bufs[k % WOVEN_BUFS]
+            width = WOVEN_ROWS * C
+            for i in range(3):
+                nc.sync.dma_start(
+                    out=woven[i:P:WEAVE, :, 0 : count * width],
+                    in_=woven_views[i][:, :, first * width : (first + count) * width],
+                )
+            for u in range(count):
+                live["woven", first + u] = (woven, u * width)
+
+        def load_plain(first):
+            plain = loads.tile([P, 3, PLAIN_UNITS * C], BF16)
+            cols = slice((WOVEN + first) * C, (WOVEN + first + PLAIN_UNITS) * C)
+            for i in range(3):
+                nc.sync.dma_start(out=plain[:, i, :], in_=plain_views[i][:, cols])
+            for u in range(PLAIN_UNITS):
+                live["plain", first + u] = plain[:, :, u * C : (u + 1) * C]
+
+        half = WOVEN_ROWS * C
+
+        def clear(engine, i, sets, start, width):
+            engine.memset(woven_bufs[i][:].bitcast(U32)[:, sets, start // 2 : (start + width) // 2], 0)
+
+        every = slice(0, SETS)
+        clear(nc.vector, 0, slice(0, 2), 0, half)
+        clear(nc.gpsimd, 0, slice(2, SETS), 0, half)
         w0_raw = stage.tile([P, PACK, MID], BF16)
         nc.scalar.dma_start(out=w0_raw[:], in_=W0.rearrange("(t p) n -> p t n", p=P))
         b0_rows = stage.tile([P, P], BF16)
-        nc.vector.memset(b0_rows[:], 0.0)
+        nc.vector.memset(b0_rows[:].bitcast(U32), 0)
         nc.scalar.dma_start(out=b0_rows[0:PACK, :], in_=b0.rearrange("(m p) -> m p", p=P))
-        load_unit(0)
-        load_unit(1)
-        w1_raw = stage.tile([P, PACK, MID], BF16)
-        nc.sync.dma_start(out=w1_raw[:], in_=W1.rearrange("(t p) n -> p t n", p=P))
-        b1_bf16 = stage.tile([P, MID], BF16)
-        nc.sync.dma_start(out=b1_bf16[:], in_=b1.partition_broadcast(P))
-        load_unit(2)
-
+        load_woven(0)
+        load_plain(0)
+        warm = stage.tile([P, 1], F32)
+        nc.vector.memset(warm[:], 0.0)
+        nc.scalar.activation(out=warm[:], in_=warm[:], func=ACT.Gelu_apprx_tanh)
         ident = keep.tile([P, P], BF16)
         make_identity(nc, ident[:])
-        add_pairs = keep.tile([P, P // 2], BF16)
-        ident_pairs = ident[:].rearrange("k (n j) -> k n j", j=2)
-        nc.vector.tensor_tensor(out=add_pairs[:], in0=ident_pairs[:, :, 0], in1=ident_pairs[:, :, 1], op=ALU.add)
+        clear(nc.vector, 1, every, 0, half)
+        load_woven(1)
+        clear(nc.vector, 1, every, half, half)
+        w1_raw = stage.tile([P, PACK, MID], BF16)
+        nc.sync.dma_start(out=w1_raw[:], in_=W1.rearrange("(t p) n -> p t n", p=P))
+        b1_rows = stage.tile([P, MID], BF16)
+        nc.gpsimd.memset(b1_rows[:].bitcast(U32), 0)
+        nc.sync.dma_start(out=b1_rows[0:1, :], in_=b1.rearrange("(o n) -> o n", o=1))
+        clear(nc.gpsimd, 2, every, 0, 2 * half)
+        load_woven(2)
+        load_plain(2)
+
+        ident_f32 = keep.tile([P, P], F32)
+        nc.vector.tensor_copy(out=ident_f32[:], in_=ident[:])
+        weave = keep.tile([P, STREAMS, 2], BF16)
+        places = ident[:].rearrange("k (n i) -> k n i", i=WEAVE)
+        q_places = stage.tile([P, STREAMS], BF16)
+        nc.vector.tensor_tensor(out=q_places[:], in0=places[:, :, 1], in1=places[:, :, 2], op=ALU.add)
+        nc.vector.tensor_tensor(out=weave[:, :, 0], in0=places[:, :, 0], in1=q_places[:], op=ALU.subtract)
+        nc.vector.tensor_scalar_mul(out=weave[:, :, 1], in0=q_places[:], scalar1=-1.0)
+        ones = stage.tile([P, P], BF16)
+        nc.vector.memset(ones[:], 1.0)
 
         sample_t = []
-        for i in range(SAMPLE_BUFS):
-            sample_zero = keep.tile([P, 2, 2, UNIT], BF16, name="sample_zero%d" % i)
-            nc.vector.memset(sample_zero[:, 1, :, :], 0.0)
+        for i in range(2):
+            sample_zero = keep.tile([P, 2, 2, P], BF16, name="sample_zero%d" % i)
+            nc.vector.memset(sample_zero[:, 1, :, :].rearrange("p c n -> p (c n)").bitcast(U32), 0)
             sample_t.append(sample_zero)
 
-        w0_codes, w0_scales = quantise_weight(nc, stage, keep, w0_raw, 2, "w0")
+        def quantise_weight(grouped, name):
+            codes = keep.tile([P, MID], U32, name=name + "_codes", align_bytes=64)
+            scales = keep.tile([P, MID], U8, name=name + "_scales", align_bytes=64)
+            nc.vector.quantize_mx(
+                out=codes[:].bitcast(FP8X4),
+                scales=scales[:],
+                in_=grouped[:].rearrange("p n t -> p (n t)"),
+            )
+            return codes, scales
 
-        b0_ps = ps_sample.tile([P, P], BF16, tag="sample_ps")
-        nc.tensor.transpose(b0_ps[:], b0_rows[:], ident[:])
+        nc.vector.tensor_scalar_mul(out=w0_raw[:, 2:4, :], in0=w0_raw[:, 2:4, :], scalar1=-1.0)
+        w0_grouped = stage.tile([P, MID, PACK], BF16, align_bytes=64)
+        nc.vector.tensor_copy(
+            out=w0_grouped[:].rearrange("p n (c h) -> p n c h", h=2),
+            in_=w0_raw[:].rearrange("p (h c) n -> p n c h", h=2),
+        )
+        w0_codes, w0_scales = quantise_weight(w0_grouped, "w0")
+
+        b0_ps = ps_x.tile([P, 2 * P, PACK], BF16, tag="x_ab")
+        b0_turned = b0_ps[:].rearrange("p n t -> p (n t)")[:, 0:P]
+        nc.tensor.transpose(b0_turned, b0_rows[:], ident[:])
         b0_cols = keep.tile([P, PACK], F32)
-        nc.vector.tensor_copy(out=b0_cols[:], in_=b0_ps[:, 0:PACK])
+        nc.vector.tensor_copy(out=b0_cols[:], in_=b0_turned[:, 0:PACK])
 
         grouped = keep.tile([P, 2, UNIT, PACK], BF16, align_bytes=64)
         b1_all = keep.tile([P, MID], F32)
 
-        def channels(j, c):
-            return slice(j * C + c * P, j * C + (c + 1) * P)
+        def add_plain(unit):
+            plain = live["plain", unit]
+            q_row = work.tile([P, C], F32)
+            nc.gpsimd.tensor_tensor(out=q_row[:], in0=plain[:, 1, :], in1=plain[:, 2, :], op=ALU.add)
+            live["q_row", unit] = q_row
 
-        def turn_sample(unit):
-            sample_ps = ps_sample.tile([P, 2, UNIT], BF16, tag="sample_ps")
-            for j in range(UNIT_ROWS):
-                for c in range(2):
-                    nc.tensor.transpose(sample_ps[:, c, j * P : (j + 1) * P], live["sample", unit][:, channels(j, c)], ident[:])
-            nc.scalar.copy(out=sample_t[unit % SAMPLE_BUFS][:, 0, :, :], in_=sample_ps[:])
+        def turn_plain(unit):
+            plain_ps = ps_x.tile([P, MID], F32)
+            q_ps = plain_ps[:, 0:C]
+            sample_ps = plain_ps[:, C : C + P].bitcast(BF16)
+            for c in range(2):
+                cols = slice(c * P, (c + 1) * P)
+                nc.tensor.transpose(q_ps[:, cols], live["q_row", unit][:, cols], ident_f32[:])
+            for c in range(2):
+                cols = slice(c * P, (c + 1) * P)
+                nc.tensor.transpose(sample_ps[:, cols], live["plain", unit][:, 0, cols], ident[:])
+            live["plain_ps", unit] = (q_ps, sample_ps)
 
-        def turn_query(unit, half):
-            q_ps = ps_q.tile([P, 2, HALF], F32)
-            for jj in range(2):
-                for c in range(2):
-                    for a in range(2):
-                        n0 = jj * P + a * (P // 2)
+        def copy_sample(unit):
+            sample_ps = live["plain_ps", unit][1]
+            nc.scalar.copy(
+                out=sample_t[unit % 2][:, 0, :, :], in_=sample_ps.rearrange("p (c n) -> p c n", c=2)
+            )
+
+        def weave_rows(unit, rows, name):
+            woven, start = live["woven", unit]
+            x_ps = ps_x.tile([P, 2 * P, PACK], BF16, name=name, tag=name)
+            for jj, j in enumerate(rows):
+                for r in range(SETS):
+                    n0 = jj * P + r * STREAMS
+                    for c in range(2):
+                        first = start + j * C + c * P
                         nc.tensor.matmul(
-                            out=q_ps[:, c, n0 : n0 + P // 2],
-                            lhsT=live["query_pos", unit][:, a, channels(2 * half + jj, c)],
-                            rhs=add_pairs[:],
+                            out=x_ps[:, n0 : n0 + STREAMS, 2 * c : 2 * c + 2],
+                            lhsT=woven[:, r, first : first + P],
+                            rhs=weave[:],
                             start=True,
                             stop=True,
                         )
-            live["q_ps", unit, half] = q_ps
+            live[name, unit] = x_ps
 
-        def make_x(unit, half):
-            tokens = slice(half * HALF, (half + 1) * HALF)
+        def copy_x(unit, rows, name):
+            tokens = slice(rows[0] * P, (rows[-1] + 1) * P)
+            nc.vector.tensor_copy(out=grouped[:, 0, tokens, :], in_=live[name, unit][:, 0 : len(rows) * P, :])
+
+        def make_plain_x(unit):
+            tokens = slice(WOVEN_ROWS * P, UNIT)
+            q_ps = live["plain_ps", unit][0]
             nc.vector.tensor_tensor(
-                out=grouped[:, 0, tokens, :].rearrange("p n (u c) -> p n u c", c=2),
-                in0=sample_t[unit % SAMPLE_BUFS][:, :, :, tokens].rearrange("p u c n -> p n u c"),
-                in1=live["q_ps", unit, half][:].rearrange("p c n -> p n c").unsqueeze(2).to_broadcast([P, HALF, 2, 2]),
+                out=grouped[:, 0, tokens, :].rearrange("p n (c h) -> p n c h", h=2),
+                in0=sample_t[unit % 2][:].rearrange("p h c n -> p n c h"),
+                in1=q_ps.rearrange("p (c n) -> p n c", c=2).unsqueeze(3).to_broadcast([P, P, 2, 2]),
                 op=ALU.subtract,
             )
 
@@ -186,16 +254,19 @@ def tile_samplequerymessagepassing_pa_t_kernel(
                 scale=1.0,
             )
 
-        def regroup_h(unit, half):
-            tokens = slice(half * HALF, (half + 1) * HALF)
+        def lay_words(out, planes):
             nc.gpsimd.tensor_scalar(
-                out=grouped[:, 1, tokens, :],
-                in0=live["h_planes", unit][:, :, tokens].rearrange("p t n -> p n t"),
+                out=out,
+                in0=planes.rearrange("p t n -> p n t"),
                 scalar1=1.0,
                 scalar2=0.0,
                 op0=ALU.mult,
                 op1=ALU.add,
             )
+
+        def regroup_h(unit, half_unit):
+            tokens = slice(half_unit * (UNIT // 2), (half_unit + 1) * (UNIT // 2))
+            lay_words(grouped[:, 1, tokens, :], live["h_planes", unit][:, :, tokens])
 
         def layer2(unit, j):
             h_codes, h_scales = live["h", unit]
@@ -221,55 +292,66 @@ def tile_samplequerymessagepassing_pa_t_kernel(
                 out=live["biased", unit][:, j, :], in0=live["out_ps", unit, j][:], in1=b1_all[:], op=ALU.add
             )
 
-        def copy_last(unit):
-            j = UNIT_ROWS - 1
-            nc.scalar.copy(out=live["biased", unit][:, j, :], in_=live["out_ps", unit, j][:])
-
-        def add_b1_last(unit):
-            last = live["biased", unit][:, UNIT_ROWS - 1, :]
-            nc.gpsimd.tensor_tensor(out=last, in0=last, in1=b1_all[:], op=ALU.add)
-
         def finish(unit, j0):
             result = stores.tile([P, 2, MID], F32)
             nc.scalar.activation(out=result[:], in_=live["biased", unit][:, j0 : j0 + 2, :], func=ACT.Gelu_apprx_tanh)
-            row0 = unit * UNIT_ROWS + j0
-            nc.sync.dma_start(out=out_rows[:, row0 : row0 + 2, :], in_=result[:])
+            row0 = unit * WOVEN_ROWS + j0
+            row1 = row0 + 1 if j0 == 0 else WOVEN + unit
+            nc.sync.dma_start(out=out_rows[:, row0 : row1 + 1 : row1 - row0, :], in_=result[:])
 
-        with tc.manual_schedule():
-            for step in range(-1, UNITS + 4):
-                if is_unit(step - 4):
-                    finish(step - 4, 2)
-                if is_unit(step + 1):
-                    turn_sample(step + 1)
-                for half in range(2):
-                    if is_unit(step):
-                        make_x(step, half)
-                    if is_unit(step + 1):
-                        turn_query(step + 1, half)
-                if is_unit(step - 3):
-                    for j in range(VECTOR_ROWS):
-                        add_b1(step - 3, j)
-                        if j + OUT_BANKS < UNIT_ROWS:
-                            layer2(step - 3, j + OUT_BANKS)
-                        if j == 1:
-                            finish(step - 3, 0)
-                    copy_last(step - 3)
-                if is_unit(step) or is_unit(step - 2):
-                    quantise(step, step - 2)
-                if is_unit(step - 1):
-                    regroup_h(step - 1, 0)
-                if is_unit(step - 3):
-                    add_b1_last(step - 3)
-                if is_unit(step - 1):
-                    regroup_h(step - 1, 1)
-                if step == 0:
-                    live["w1"] = quantise_weight(nc, stage, keep, w1_raw, 0, "w1")
-                    nc.vector.tensor_copy(out=b1_all[:], in_=b1_bf16[:])
-                for m in range(PACK):
-                    if m == H_BANKS and is_unit(step - 2):
-                        for j in range(OUT_BANKS):
-                            layer2(step - 2, j)
-                    if is_unit(step):
-                        layer1(step, m)
-                if is_unit(step + PREFETCH):
-                    load_unit(step + PREFETCH)
+        w1_grouped = stage.tile([P, MID, PACK], BF16, align_bytes=64)
+
+        def regroup_w1():
+            lay_words(w1_grouped[:], w1_raw[:])
+
+        def prepare_layer2():
+            live["w1"] = quantise_weight(w1_grouped, "w1")
+            b1_ps = ps_out.tile([P, MID], F32, tag="out_ps")
+            nc.tensor.matmul(out=b1_ps[:], lhsT=ones[:], rhs=b1_rows[:], start=True, stop=True)
+            nc.vector.tensor_copy(out=b1_all[:], in_=b1_ps[:])
+
+        for step in range(-3, UNITS + 4):
+            if is_unit(step) or is_unit(step - 2):
+                quantise(step, step - 2)
+            if is_unit(step - 3):
+                add_b1(step - 3, UNIT_ROWS - 1)
+            if is_unit(step + 1):
+                copy_x(step + 1, (0, 1), "x_ab")
+                copy_x(step + 1, (2,), "x_c")
+                make_plain_x(step + 1)
+            if is_unit(step + 3):
+                add_plain(step + 3)
+            if step == -2:
+                clear(nc.gpsimd, 0, every, half, half)
+            if is_unit(step - 1):
+                regroup_h(step - 1, 0)
+                regroup_h(step - 1, 1)
+            for m in range(PACK):
+                if m == H_BANKS and is_unit(step - 2):
+                    for j in range(OUT_BANKS):
+                        layer2(step - 2, j)
+                if is_unit(step):
+                    layer1(step, m)
+            if step == 0:
+                regroup_w1()
+            if step == 1:
+                prepare_layer2()
+            if is_unit(step - 3):
+                finish(step - 3, 2)
+            if is_unit(step + 2):
+                turn_plain(step + 2)
+                copy_sample(step + 2)
+                weave_rows(step + 2, (0, 1), "x_ab")
+                weave_rows(step + 2, (2,), "x_c")
+            if is_unit(step - 2):
+                for j in range(OUT_BANKS):
+                    add_b1(step - 2, j)
+                    if j == 0:
+                        layer2(step - 2, UNIT_ROWS - 1)
+                finish(step - 2, 0)
+            for k in range(WOVEN_BUFS, len(CHUNKS)):
+                first, count = CHUNKS[k - WOVEN_BUFS]
+                if step == first + count - 1 - 1:
+                    load_woven(k)
+            if step >= -2 and step % 2 == 0 and is_unit(step + 6):
+                load_plain(step + 6)

@@ -50,8 +50,8 @@ def tile_samplequerymessagepassing_pa_t_kernel(
         keep = ctx.enter_context(tc.tile_pool(name="keep", bufs=1))
         stage = ctx.enter_context(tc.tile_pool(name="stage", bufs=1))
         loads = ctx.enter_context(tc.tile_pool(name="loads", bufs=3))
-        work = ctx.enter_context(tc.tile_pool(name="work", bufs=2))
-        stores = ctx.enter_context(tc.tile_pool(name="stores", bufs=3))
+        work = ctx.enter_context(tc.tile_pool(name="work", bufs=3))
+        stores = ctx.enter_context(tc.tile_pool(name="stores", bufs=6))
         ps_x = ctx.enter_context(tc.psum_pool(name="ps_x", bufs=1))
         ps_h = ctx.enter_context(tc.psum_pool(name="ps_h", bufs=H_BANKS))
         ps_out = ctx.enter_context(tc.psum_pool(name="ps_out", bufs=OUT_BANKS))
@@ -61,14 +61,15 @@ def tile_samplequerymessagepassing_pa_t_kernel(
         def is_unit(unit):
             return 0 <= unit < UNITS
 
-        woven_bufs = []
-        for i in range(WOVEN_BUFS):
-            woven = keep.tile([P, SETS, 2 * WOVEN_ROWS * C], BF16, name="woven%d" % i)
-            woven_bufs.append(woven)
+        woven_tiles = []
+        for i in range(2 + WOVEN_BUFS):
+            units = CHUNKS[i][1]
+            woven = keep.tile([P, SETS, units * WOVEN_ROWS * C], BF16, name="woven%d" % i)
+            woven_tiles.append(woven)
 
         def load_woven(k):
             first, count = CHUNKS[k]
-            woven = woven_bufs[k % WOVEN_BUFS]
+            woven = woven_tiles[k if k < 2 else 2 + (k - 2) % WOVEN_BUFS]
             width = WOVEN_ROWS * C
             for i in range(3):
                 nc.sync.dma_start(
@@ -86,14 +87,11 @@ def tile_samplequerymessagepassing_pa_t_kernel(
             for u in range(PLAIN_UNITS):
                 live["plain", first + u] = plain[:, :, u * C : (u + 1) * C]
 
-        half = WOVEN_ROWS * C
+        def clear(engine, i, sets):
+            engine.memset(woven_tiles[i][:].bitcast(U32)[:, sets, :], 0)
 
-        def clear(engine, i, sets, start, width):
-            engine.memset(woven_bufs[i][:].bitcast(U32)[:, sets, start // 2 : (start + width) // 2], 0)
-
-        every = slice(0, SETS)
-        clear(nc.vector, 0, slice(0, 2), 0, half)
-        clear(nc.gpsimd, 0, slice(2, SETS), 0, half)
+        clear(nc.vector, 0, slice(0, 2))
+        clear(nc.gpsimd, 0, slice(2, SETS))
         w0_raw = stage.tile([P, PACK, MID], BF16)
         nc.scalar.dma_start(out=w0_raw[:], in_=W0.rearrange("(t p) n -> p t n", p=P))
         b0_rows = stage.tile([P, P], BF16)
@@ -106,17 +104,18 @@ def tile_samplequerymessagepassing_pa_t_kernel(
         nc.scalar.activation(out=warm[:], in_=warm[:], func=ACT.Gelu_apprx_tanh)
         ident = keep.tile([P, P], BF16)
         make_identity(nc, ident[:])
-        clear(nc.vector, 1, every, 0, half)
+        clear(nc.vector, 1, slice(0, SETS))
         load_woven(1)
-        clear(nc.vector, 1, every, half, half)
         w1_raw = stage.tile([P, PACK, MID], BF16)
         nc.sync.dma_start(out=w1_raw[:], in_=W1.rearrange("(t p) n -> p t n", p=P))
         b1_rows = stage.tile([P, MID], BF16)
         nc.gpsimd.memset(b1_rows[:].bitcast(U32), 0)
         nc.sync.dma_start(out=b1_rows[0:1, :], in_=b1.rearrange("(o n) -> o n", o=1))
-        clear(nc.gpsimd, 2, every, 0, 2 * half)
+        clear(nc.gpsimd, 2, slice(0, SETS))
         load_woven(2)
         load_plain(2)
+        for i in range(3, 2 + WOVEN_BUFS):
+            clear(nc.gpsimd, i, slice(0, SETS))
 
         ident_f32 = keep.tile([P, P], F32)
         nc.vector.tensor_copy(out=ident_f32[:], in_=ident[:])
@@ -153,8 +152,8 @@ def tile_samplequerymessagepassing_pa_t_kernel(
         )
         w0_codes, w0_scales = quantise_weight(w0_grouped, "w0")
 
-        b0_ps = ps_x.tile([P, 2 * P, PACK], BF16, tag="x_ab")
-        b0_turned = b0_ps[:].rearrange("p n t -> p (n t)")[:, 0:P]
+        b0_ps = ps_out.tile([P, MID], F32, tag="out_ps")
+        b0_turned = b0_ps[:].bitcast(BF16)[:, 0:P]
         nc.tensor.transpose(b0_turned, b0_rows[:], ident[:])
         b0_cols = keep.tile([P, PACK], F32)
         nc.vector.tensor_copy(out=b0_cols[:], in_=b0_turned[:, 0:PACK])
@@ -165,7 +164,7 @@ def tile_samplequerymessagepassing_pa_t_kernel(
         def add_plain(unit):
             plain = live["plain", unit]
             q_row = work.tile([P, C], F32)
-            nc.gpsimd.tensor_tensor(out=q_row[:], in0=plain[:, 1, :], in1=plain[:, 2, :], op=ALU.add)
+            nc.vector.tensor_tensor(out=q_row[:], in0=plain[:, 1, :], in1=plain[:, 2, :], op=ALU.add)
             live["q_row", unit] = q_row
 
         def turn_plain(unit):
@@ -311,6 +310,8 @@ def tile_samplequerymessagepassing_pa_t_kernel(
             nc.vector.tensor_copy(out=b1_all[:], in_=b1_ps[:])
 
         for step in range(-3, UNITS + 4):
+            if is_unit(step + 2):
+                add_plain(step + 2)
             if is_unit(step) or is_unit(step - 2):
                 quantise(step, step - 2)
             if is_unit(step - 3):
@@ -319,10 +320,6 @@ def tile_samplequerymessagepassing_pa_t_kernel(
                 copy_x(step + 1, (0, 1), "x_ab")
                 copy_x(step + 1, (2,), "x_c")
                 make_plain_x(step + 1)
-            if is_unit(step + 3):
-                add_plain(step + 3)
-            if step == -2:
-                clear(nc.gpsimd, 0, every, half, half)
             if is_unit(step - 1):
                 regroup_h(step - 1, 0)
                 regroup_h(step - 1, 1)
@@ -339,19 +336,18 @@ def tile_samplequerymessagepassing_pa_t_kernel(
             if is_unit(step - 3):
                 finish(step - 3, 2)
             if is_unit(step + 2):
-                turn_plain(step + 2)
-                copy_sample(step + 2)
                 weave_rows(step + 2, (0, 1), "x_ab")
                 weave_rows(step + 2, (2,), "x_c")
+                turn_plain(step + 2)
+                copy_sample(step + 2)
             if is_unit(step - 2):
                 for j in range(OUT_BANKS):
                     add_b1(step - 2, j)
                     if j == 0:
                         layer2(step - 2, UNIT_ROWS - 1)
                 finish(step - 2, 0)
-            for k in range(WOVEN_BUFS, len(CHUNKS)):
-                first, count = CHUNKS[k - WOVEN_BUFS]
-                if step == first + count - 1 - 1:
+            for k in range(3, len(CHUNKS)):
+                if step == CHUNKS[k][0] - 2 * WOVEN_BUFS:
                     load_woven(k)
             if step >= -2 and step % 2 == 0 and is_unit(step + 6):
                 load_plain(step + 6)

@@ -335,17 +335,17 @@ def tile_samplequerymessagepassing_pa_t_kernel(
                 prepare_layer2()
             if is_unit(step - 3):
                 finish(step - 3, 2)
-            if is_unit(step + 2):
-                weave_rows(step + 2, (0, 1), "x_ab")
-                weave_rows(step + 2, (2,), "x_c")
-                turn_plain(step + 2)
-                copy_sample(step + 2)
             if is_unit(step - 2):
                 for j in range(OUT_BANKS):
                     add_b1(step - 2, j)
                     if j == 0:
                         layer2(step - 2, UNIT_ROWS - 1)
                 finish(step - 2, 0)
+            if is_unit(step + 2):
+                weave_rows(step + 2, (0, 1), "x_ab")
+                weave_rows(step + 2, (2,), "x_c")
+                turn_plain(step + 2)
+                copy_sample(step + 2)
             for k in range(3, len(CHUNKS)):
                 if step == CHUNKS[k][0] - 2 * WOVEN_BUFS:
                     load_woven(k)

@@ -117,8 +117,6 @@ def tile_samplequerymessagepassing_pa_t_kernel(
         for i in range(3, 2 + WOVEN_BUFS):
             clear(nc.gpsimd, i, slice(0, SETS))
 
-        ident_f32 = keep.tile([P, P], F32)
-        nc.vector.tensor_copy(out=ident_f32[:], in_=ident[:])
         weave = keep.tile([P, STREAMS, 2], BF16)
         places = ident[:].rearrange("k (n i) -> k n i", i=WEAVE)
         q_places = stage.tile([P, STREAMS], BF16)
@@ -128,11 +126,11 @@ def tile_samplequerymessagepassing_pa_t_kernel(
         ones = stage.tile([P, P], BF16)
         nc.vector.memset(ones[:], 1.0)
 
-        sample_t = []
-        for i in range(2):
-            sample_zero = keep.tile([P, 2, 2, P], BF16, name="sample_zero%d" % i)
-            nc.vector.memset(sample_zero[:, 1, :, :].rearrange("p c n -> p (c n)").bitcast(U32), 0)
-            sample_t.append(sample_zero)
+        zeros = stage.tile([P, P], BF16)
+        nc.vector.memset(zeros[:].bitcast(U32), 0)
+        plain_ps = ps_x.tile([P, 4, 2, P], BF16)
+        for c in range(2):
+            nc.tensor.transpose(plain_ps[:, 1, c, :], zeros[:], ident[:])
 
         def quantise_weight(grouped, name):
             codes = keep.tile([P, MID], U32, name=name + "_codes", align_bytes=64)
@@ -158,32 +156,25 @@ def tile_samplequerymessagepassing_pa_t_kernel(
         b0_cols = keep.tile([P, PACK], F32)
         nc.vector.tensor_copy(out=b0_cols[:], in_=b0_turned[:, 0:PACK])
 
-        grouped = keep.tile([P, 2, UNIT, PACK], BF16, align_bytes=64)
+        grouped_tiles = []
+        for i in range(2):
+            grouped = keep.tile([P, 2, UNIT, PACK], BF16, name="grouped%d" % i, align_bytes=64)
+            grouped_tiles.append(grouped)
         b1_all = keep.tile([P, MID], F32)
 
-        def add_plain(unit):
-            plain = live["plain", unit]
-            q_row = work.tile([P, C], F32)
-            nc.vector.tensor_tensor(out=q_row[:], in0=plain[:, 1, :], in1=plain[:, 2, :], op=ALU.add)
-            live["q_row", unit] = q_row
-
         def turn_plain(unit):
-            plain_ps = ps_x.tile([P, MID], F32)
-            q_ps = plain_ps[:, 0:C]
-            sample_ps = plain_ps[:, C : C + P].bitcast(BF16)
-            for c in range(2):
-                cols = slice(c * P, (c + 1) * P)
-                nc.tensor.transpose(q_ps[:, cols], live["q_row", unit][:, cols], ident_f32[:])
-            for c in range(2):
-                cols = slice(c * P, (c + 1) * P)
-                nc.tensor.transpose(sample_ps[:, cols], live["plain", unit][:, 0, cols], ident[:])
-            live["plain_ps", unit] = (q_ps, sample_ps)
+            for i, place in ((2, 3), (1, 2), (0, 0)):
+                for c in range(2):
+                    cols = slice(c * P, (c + 1) * P)
+                    nc.tensor.transpose(plain_ps[:, place, c, :], live["plain", unit][:, i, cols], ident[:])
+            pos_t = work.tile([P, 2, P], BF16)
+            nc.scalar.copy(out=pos_t[:], in_=plain_ps[:, 3, :, :])
+            live["pos_t", unit] = pos_t
 
-        def copy_sample(unit):
-            sample_ps = live["plain_ps", unit][1]
-            nc.scalar.copy(
-                out=sample_t[unit % 2][:, 0, :, :], in_=sample_ps.rearrange("p (c n) -> p c n", c=2)
-            )
+        def add_plain(unit):
+            q_t = work.tile([P, 2, P], F32)
+            nc.vector.tensor_tensor(out=q_t[:], in0=plain_ps[:, 2, :, :], in1=live["pos_t", unit][:], op=ALU.add)
+            live["q_t", unit] = q_t
 
         def weave_rows(unit, rows, name):
             woven, start = live["woven", unit]
@@ -204,19 +195,19 @@ def tile_samplequerymessagepassing_pa_t_kernel(
 
         def copy_x(unit, rows, name):
             tokens = slice(rows[0] * P, (rows[-1] + 1) * P)
-            nc.vector.tensor_copy(out=grouped[:, 0, tokens, :], in_=live[name, unit][:, 0 : len(rows) * P, :])
+            nc.vector.tensor_copy(out=grouped_tiles[unit % 2][:, 0, tokens, :], in_=live[name, unit][:, 0 : len(rows) * P, :])
 
         def make_plain_x(unit):
             tokens = slice(WOVEN_ROWS * P, UNIT)
-            q_ps = live["plain_ps", unit][0]
             nc.vector.tensor_tensor(
-                out=grouped[:, 0, tokens, :].rearrange("p n (c h) -> p n c h", h=2),
-                in0=sample_t[unit % 2][:].rearrange("p h c n -> p n c h"),
-                in1=q_ps.rearrange("p (c n) -> p n c", c=2).unsqueeze(3).to_broadcast([P, P, 2, 2]),
+                out=grouped_tiles[unit % 2][:, 0, tokens, :].rearrange("p n (c h) -> p n c h", h=2),
+                in0=plain_ps[:, 0:2, :, :].rearrange("p h c n -> p n c h"),
+                in1=live["q_t", unit][:].rearrange("p c n -> p n c").unsqueeze(3).to_broadcast([P, P, 2, 2]),
                 op=ALU.subtract,
             )
 
         def quantise(x_unit, h_unit):
+            grouped = grouped_tiles[x_unit % 2]
             first = 0 if is_unit(x_unit) else 1
             last = 2 if is_unit(h_unit) else 1
             codes = work.tile([P, 2, UNIT], U32, align_bytes=64)
@@ -265,7 +256,7 @@ def tile_samplequerymessagepassing_pa_t_kernel(
 
         def regroup_h(unit, half_unit):
             tokens = slice(half_unit * (UNIT // 2), (half_unit + 1) * (UNIT // 2))
-            lay_words(grouped[:, 1, tokens, :], live["h_planes", unit][:, :, tokens])
+            lay_words(grouped_tiles[(unit + 1) % 2][:, 1, tokens, :], live["h_planes", unit][:, :, tokens])
 
         def layer2(unit, j):
             h_codes, h_scales = live["h", unit]
@@ -309,43 +300,44 @@ def tile_samplequerymessagepassing_pa_t_kernel(
             nc.tensor.matmul(out=b1_ps[:], lhsT=ones[:], rhs=b1_rows[:], start=True, stop=True)
             nc.vector.tensor_copy(out=b1_all[:], in_=b1_ps[:])
 
-        for step in range(-3, UNITS + 4):
-            if is_unit(step + 2):
-                add_plain(step + 2)
-            if is_unit(step) or is_unit(step - 2):
-                quantise(step, step - 2)
-            if is_unit(step - 3):
-                add_b1(step - 3, UNIT_ROWS - 1)
+        for step in range(-2, UNITS + 5):
+            if is_unit(step) or is_unit(step - 3):
+                quantise(step, step - 3)
+            if is_unit(step - 4):
+                add_b1(step - 4, UNIT_ROWS - 1)
             if is_unit(step + 1):
                 copy_x(step + 1, (0, 1), "x_ab")
                 copy_x(step + 1, (2,), "x_c")
-                make_plain_x(step + 1)
+                add_plain(step + 1)
             if is_unit(step - 1):
                 regroup_h(step - 1, 0)
                 regroup_h(step - 1, 1)
             for m in range(PACK):
-                if m == H_BANKS and is_unit(step - 2):
+                if m == H_BANKS and is_unit(step - 3):
                     for j in range(OUT_BANKS):
-                        layer2(step - 2, j)
+                        layer2(step - 3, j)
                 if is_unit(step):
                     layer1(step, m)
             if step == 0:
                 regroup_w1()
             if step == 1:
                 prepare_layer2()
+            if is_unit(step - 4):
+                finish(step - 4, 2)
             if is_unit(step - 3):
-                finish(step - 3, 2)
-            if is_unit(step - 2):
-                for j in range(OUT_BANKS):
-                    add_b1(step - 2, j)
-                    if j == 0:
-                        layer2(step - 2, UNIT_ROWS - 1)
-                finish(step - 2, 0)
+                add_b1(step - 3, 0)
+                layer2(step - 3, UNIT_ROWS - 1)
+            if is_unit(step + 1):
+                make_plain_x(step + 1)
+            if is_unit(step - 3):
+                for j in range(1, OUT_BANKS):
+                    add_b1(step - 3, j)
             if is_unit(step + 2):
                 weave_rows(step + 2, (0, 1), "x_ab")
                 weave_rows(step + 2, (2,), "x_c")
                 turn_plain(step + 2)
-                copy_sample(step + 2)
+            if is_unit(step - 3):
+                finish(step - 3, 0)
             for k in range(3, len(CHUNKS)):
                 if step == CHUNKS[k][0] - 2 * WOVEN_BUFS:
                     load_woven(k)

@@ -20,16 +20,30 @@ ROWS = TOKENS // P
 UNIT_ROWS = 4
 UNIT = UNIT_ROWS * P
 UNITS = ROWS // UNIT_ROWS
-WOVEN_ROWS = 3
-WOVEN = WOVEN_ROWS * UNITS
+PLAIN_UNITS = range(1, UNITS - 1)
 STREAMS = 32
 WEAVE = 4
 SETS = P // STREAMS
 H_BANKS = 2
 OUT_BANKS = 3
-PLAIN_UNITS = 2
+PLAIN_LOAD = 2
 WOVEN_BUFS = 3
-CHUNKS = [(0, 1), (1, 1)] + [(u, 2) for u in range(2, UNITS, 2)]
+CHUNKS = [(0, 1), (1, 1)] + [(u, 2) for u in range(2, UNITS - 2, 2)] + [(UNITS - 2, 1), (UNITS - 1, 1)]
+
+
+def woven_rows(unit):
+    return UNIT_ROWS - (unit in PLAIN_UNITS)
+
+
+def first_row(unit):
+    return sum(woven_rows(u) for u in range(unit))
+
+
+def row_of(unit, j):
+    if j < woven_rows(unit):
+        return first_row(unit) + j
+    return first_row(UNITS) + PLAIN_UNITS.index(unit)
+
 
 FLOPS = 2 * TOKENS * (2 * C * MID + MID * MID)
 
@@ -63,28 +77,27 @@ def tile_samplequerymessagepassing_pa_t_kernel(
 
         woven_tiles = []
         for i in range(2 + WOVEN_BUFS):
-            units = CHUNKS[i][1]
-            woven = keep.tile([P, SETS, units * WOVEN_ROWS * C], BF16, name="woven%d" % i)
+            first, count = CHUNKS[i]
+            rows = first_row(first + count) - first_row(first)
+            woven = keep.tile([P, SETS, rows * C], BF16, name="woven%d" % i)
             woven_tiles.append(woven)
 
         def load_woven(k):
             first, count = CHUNKS[k]
             woven = woven_tiles[k if k < 2 else 2 + (k - 2) % WOVEN_BUFS]
-            width = WOVEN_ROWS * C
+            start, stop = first_row(first) * C, first_row(first + count) * C
             for i in range(3):
-                nc.sync.dma_start(
-                    out=woven[i:P:WEAVE, :, 0 : count * width],
-                    in_=woven_views[i][:, :, first * width : (first + count) * width],
-                )
-            for u in range(count):
-                live["woven", first + u] = (woven, u * width)
+                nc.sync.dma_start(out=woven[i:P:WEAVE, :, 0 : stop - start], in_=woven_views[i][:, :, start:stop])
+            for u in range(first, first + count):
+                live["woven", u] = (woven, first_row(u) * C - start)
 
         def load_plain(first):
-            plain = loads.tile([P, 3, PLAIN_UNITS * C], BF16)
-            cols = slice((WOVEN + first) * C, (WOVEN + first + PLAIN_UNITS) * C)
+            plain = loads.tile([P, 3, PLAIN_LOAD * C], BF16)
+            start = row_of(first, UNIT_ROWS - 1) * C
+            cols = slice(start, start + PLAIN_LOAD * C)
             for i in range(3):
                 nc.sync.dma_start(out=plain[:, i, :], in_=plain_views[i][:, cols])
-            for u in range(PLAIN_UNITS):
+            for u in range(PLAIN_LOAD):
                 live["plain", first + u] = plain[:, :, u * C : (u + 1) * C]
 
         def clear(engine, i, sets):
@@ -98,7 +111,6 @@ def tile_samplequerymessagepassing_pa_t_kernel(
         nc.vector.memset(b0_rows[:].bitcast(U32), 0)
         nc.scalar.dma_start(out=b0_rows[0:PACK, :], in_=b0.rearrange("(m p) -> m p", p=P))
         load_woven(0)
-        load_plain(0)
         warm = stage.tile([P, 1], F32)
         nc.vector.memset(warm[:], 0.0)
         nc.scalar.activation(out=warm[:], in_=warm[:], func=ACT.Gelu_apprx_tanh)
@@ -106,6 +118,7 @@ def tile_samplequerymessagepassing_pa_t_kernel(
         make_identity(nc, ident[:])
         clear(nc.vector, 1, slice(0, SETS))
         load_woven(1)
+        load_plain(1)
         w1_raw = stage.tile([P, PACK, MID], BF16)
         nc.sync.dma_start(out=w1_raw[:], in_=W1.rearrange("(t p) n -> p t n", p=P))
         b1_rows = stage.tile([P, MID], BF16)
@@ -113,10 +126,10 @@ def tile_samplequerymessagepassing_pa_t_kernel(
         nc.sync.dma_start(out=b1_rows[0:1, :], in_=b1.rearrange("(o n) -> o n", o=1))
         clear(nc.gpsimd, 2, slice(0, SETS))
         load_woven(2)
-        load_plain(2)
-        for i in range(3, 2 + WOVEN_BUFS):
-            clear(nc.gpsimd, i, slice(0, SETS))
+        load_plain(3)
 
+        ident_f32 = keep.tile([P, P], F32)
+        nc.vector.tensor_copy(out=ident_f32[:], in_=ident[:])
         weave = keep.tile([P, STREAMS, 2], BF16)
         places = ident[:].rearrange("k (n i) -> k n i", i=WEAVE)
         q_places = stage.tile([P, STREAMS], BF16)
@@ -126,11 +139,11 @@ def tile_samplequerymessagepassing_pa_t_kernel(
         ones = stage.tile([P, P], BF16)
         nc.vector.memset(ones[:], 1.0)
 
-        zeros = stage.tile([P, P], BF16)
-        nc.vector.memset(zeros[:].bitcast(U32), 0)
-        plain_ps = ps_x.tile([P, 4, 2, P], BF16)
-        for c in range(2):
-            nc.tensor.transpose(plain_ps[:, 1, c, :], zeros[:], ident[:])
+        sample_t = []
+        for i in range(2):
+            sample_zero = keep.tile([P, 2, 2, P], BF16, name="sample_zero%d" % i)
+            nc.vector.memset(sample_zero[:, 1, :, :].rearrange("p c n -> p (c n)").bitcast(U32), 0)
+            sample_t.append(sample_zero)
 
         def quantise_weight(grouped, name):
             codes = keep.tile([P, MID], U32, name=name + "_codes", align_bytes=64)
@@ -162,19 +175,29 @@ def tile_samplequerymessagepassing_pa_t_kernel(
             grouped_tiles.append(grouped)
         b1_all = keep.tile([P, MID], F32)
 
-        def turn_plain(unit):
-            for i, place in ((2, 3), (1, 2), (0, 0)):
-                for c in range(2):
-                    cols = slice(c * P, (c + 1) * P)
-                    nc.tensor.transpose(plain_ps[:, place, c, :], live["plain", unit][:, i, cols], ident[:])
-            pos_t = work.tile([P, 2, P], BF16)
-            nc.scalar.copy(out=pos_t[:], in_=plain_ps[:, 3, :, :])
-            live["pos_t", unit] = pos_t
-
         def add_plain(unit):
-            q_t = work.tile([P, 2, P], F32)
-            nc.vector.tensor_tensor(out=q_t[:], in0=plain_ps[:, 2, :, :], in1=live["pos_t", unit][:], op=ALU.add)
-            live["q_t", unit] = q_t
+            plain = live["plain", unit]
+            q_row = work.tile([P, C], F32)
+            nc.gpsimd.tensor_tensor(out=q_row[:], in0=plain[:, 1, :], in1=plain[:, 2, :], op=ALU.add)
+            live["q_row", unit] = q_row
+
+        def turn_plain(unit):
+            plain_ps = ps_x.tile([P, MID], F32)
+            q_ps = plain_ps[:, 0:C]
+            sample_ps = plain_ps[:, C : C + P].bitcast(BF16)
+            for c in range(2):
+                cols = slice(c * P, (c + 1) * P)
+                nc.tensor.transpose(q_ps[:, cols], live["q_row", unit][:, cols], ident_f32[:])
+            for c in range(2):
+                cols = slice(c * P, (c + 1) * P)
+                nc.tensor.transpose(sample_ps[:, cols], live["plain", unit][:, 0, cols], ident[:])
+            live["plain_ps", unit] = (q_ps, sample_ps)
+
+        def copy_sample(unit):
+            sample_ps = live["plain_ps", unit][1]
+            nc.scalar.copy(
+                out=sample_t[unit % 2][:, 0, :, :], in_=sample_ps.rearrange("p (c n) -> p c n", c=2)
+            )
 
         def weave_rows(unit, rows, name):
             woven, start = live["woven", unit]
@@ -193,16 +216,17 @@ def tile_samplequerymessagepassing_pa_t_kernel(
                         )
             live[name, unit] = x_ps
 
-        def copy_x(unit, rows, name):
+        def copy_x(copy, unit, rows, name):
             tokens = slice(rows[0] * P, (rows[-1] + 1) * P)
-            nc.vector.tensor_copy(out=grouped_tiles[unit % 2][:, 0, tokens, :], in_=live[name, unit][:, 0 : len(rows) * P, :])
+            copy(out=grouped_tiles[unit % 2][:, 0, tokens, :], in_=live[name, unit][:, 0 : len(rows) * P, :])
 
         def make_plain_x(unit):
-            tokens = slice(WOVEN_ROWS * P, UNIT)
+            tokens = slice((UNIT_ROWS - 1) * P, UNIT)
+            q_ps = live["plain_ps", unit][0]
             nc.vector.tensor_tensor(
                 out=grouped_tiles[unit % 2][:, 0, tokens, :].rearrange("p n (c h) -> p n c h", h=2),
-                in0=plain_ps[:, 0:2, :, :].rearrange("p h c n -> p n c h"),
-                in1=live["q_t", unit][:].rearrange("p c n -> p n c").unsqueeze(3).to_broadcast([P, P, 2, 2]),
+                in0=sample_t[unit % 2][:].rearrange("p h c n -> p n c h"),
+                in1=q_ps.rearrange("p (c n) -> p n c", c=2).unsqueeze(3).to_broadcast([P, P, 2, 2]),
                 op=ALU.subtract,
             )
 
@@ -285,8 +309,7 @@ def tile_samplequerymessagepassing_pa_t_kernel(
         def finish(unit, j0):
             result = stores.tile([P, 2, MID], F32)
             nc.scalar.activation(out=result[:], in_=live["biased", unit][:, j0 : j0 + 2, :], func=ACT.Gelu_apprx_tanh)
-            row0 = unit * WOVEN_ROWS + j0
-            row1 = row0 + 1 if j0 == 0 else WOVEN + unit
+            row0, row1 = row_of(unit, j0), row_of(unit, j0 + 1)
             nc.sync.dma_start(out=out_rows[:, row0 : row1 + 1 : row1 - row0, :], in_=result[:])
 
         w1_grouped = stage.tile([P, MID, PACK], BF16, align_bytes=64)
@@ -300,18 +323,21 @@ def tile_samplequerymessagepassing_pa_t_kernel(
             nc.tensor.matmul(out=b1_ps[:], lhsT=ones[:], rhs=b1_rows[:], start=True, stop=True)
             nc.vector.tensor_copy(out=b1_all[:], in_=b1_ps[:])
 
-        for step in range(-2, UNITS + 5):
+        for step in range(-3, UNITS + 5):
             if is_unit(step) or is_unit(step - 3):
                 quantise(step, step - 3)
             if is_unit(step - 4):
                 add_b1(step - 4, UNIT_ROWS - 1)
             if is_unit(step + 1):
-                copy_x(step + 1, (0, 1), "x_ab")
-                copy_x(step + 1, (2,), "x_c")
-                add_plain(step + 1)
+                copy_x(nc.vector.tensor_copy, step + 1, range(0, 2), "x_ab")
+                copy_x(nc.scalar.copy, step + 1, range(2, woven_rows(step + 1)), "x_cd")
             if is_unit(step - 1):
                 regroup_h(step - 1, 0)
                 regroup_h(step - 1, 1)
+            if step + 3 in PLAIN_UNITS:
+                add_plain(step + 3)
+            if step < -1:
+                clear(nc.gpsimd, step + 6, slice(0, SETS))
             for m in range(PACK):
                 if m == H_BANKS and is_unit(step - 3):
                     for j in range(OUT_BANKS):
@@ -327,19 +353,21 @@ def tile_samplequerymessagepassing_pa_t_kernel(
             if is_unit(step - 3):
                 add_b1(step - 3, 0)
                 layer2(step - 3, UNIT_ROWS - 1)
-            if is_unit(step + 1):
+            if step + 1 in PLAIN_UNITS:
                 make_plain_x(step + 1)
             if is_unit(step - 3):
                 for j in range(1, OUT_BANKS):
                     add_b1(step - 3, j)
             if is_unit(step + 2):
-                weave_rows(step + 2, (0, 1), "x_ab")
-                weave_rows(step + 2, (2,), "x_c")
+                weave_rows(step + 2, range(0, 2), "x_ab")
+                weave_rows(step + 2, range(2, woven_rows(step + 2)), "x_cd")
+            if step + 2 in PLAIN_UNITS:
                 turn_plain(step + 2)
+                copy_sample(step + 2)
             if is_unit(step - 3):
                 finish(step - 3, 0)
-            for k in range(3, len(CHUNKS)):
+            for k in range(2 + 1, len(CHUNKS)):
                 if step == CHUNKS[k][0] - 2 * WOVEN_BUFS:
                     load_woven(k)
-            if step >= -2 and step % 2 == 0 and is_unit(step + 6):
+            if step >= -1 and step % 2 == 1 and step + 6 in PLAIN_UNITS:
                 load_plain(step + 6)

@@ -64,7 +64,7 @@ def tile_samplequerymessagepassing_pa_t_kernel(
         keep = ctx.enter_context(tc.tile_pool(name="keep", bufs=1))
         stage = ctx.enter_context(tc.tile_pool(name="stage", bufs=1))
         loads = ctx.enter_context(tc.tile_pool(name="loads", bufs=3))
-        work = ctx.enter_context(tc.tile_pool(name="work", bufs=3))
+        work = ctx.enter_context(tc.tile_pool(name="work", bufs=4))
         stores = ctx.enter_context(tc.tile_pool(name="stores", bufs=6))
         ps_x = ctx.enter_context(tc.psum_pool(name="ps_x", bufs=1))
         ps_h = ctx.enter_context(tc.psum_pool(name="ps_h", bufs=H_BANKS))
@@ -216,9 +216,9 @@ def tile_samplequerymessagepassing_pa_t_kernel(
                         )
             live[name, unit] = x_ps
 
-        def copy_x(copy, unit, rows, name):
+        def copy_x(unit, rows, name):
             tokens = slice(rows[0] * P, (rows[-1] + 1) * P)
-            copy(out=grouped_tiles[unit % 2][:, 0, tokens, :], in_=live[name, unit][:, 0 : len(rows) * P, :])
+            nc.vector.tensor_copy(out=grouped_tiles[unit % 2][:, 0, tokens, :], in_=live[name, unit][:, 0 : len(rows) * P, :])
 
         def make_plain_x(unit):
             tokens = slice((UNIT_ROWS - 1) * P, UNIT)
@@ -327,10 +327,11 @@ def tile_samplequerymessagepassing_pa_t_kernel(
             if is_unit(step) or is_unit(step - 3):
                 quantise(step, step - 3)
             if is_unit(step - 4):
-                add_b1(step - 4, UNIT_ROWS - 1)
+                for j in range(OUT_BANKS):
+                    add_b1(step - 4, j)
             if is_unit(step + 1):
-                copy_x(nc.vector.tensor_copy, step + 1, range(0, 2), "x_ab")
-                copy_x(nc.scalar.copy, step + 1, range(2, woven_rows(step + 1)), "x_cd")
+                copy_x(step + 1, range(0, 2), "x_ab")
+                copy_x(step + 1, range(2, woven_rows(step + 1)), "x_cd")
             if is_unit(step - 1):
                 regroup_h(step - 1, 0)
                 regroup_h(step - 1, 1)
@@ -339,33 +340,30 @@ def tile_samplequerymessagepassing_pa_t_kernel(
             if step < -1:
                 clear(nc.gpsimd, step + 6, slice(0, SETS))
             for m in range(PACK):
-                if m == H_BANKS and is_unit(step - 3):
-                    for j in range(OUT_BANKS):
-                        layer2(step - 3, j)
+                if m == H_BANKS and is_unit(step - 4):
+                    layer2(step - 4, OUT_BANKS)
                 if is_unit(step):
                     layer1(step, m)
             if step == 0:
                 regroup_w1()
-            if step == 1:
+            if step == 2:
                 prepare_layer2()
             if is_unit(step - 4):
-                finish(step - 4, 2)
-            if is_unit(step - 3):
-                add_b1(step - 3, 0)
-                layer2(step - 3, UNIT_ROWS - 1)
+                finish(step - 4, 0)
+                add_b1(step - 4, OUT_BANKS)
             if step + 1 in PLAIN_UNITS:
                 make_plain_x(step + 1)
-            if is_unit(step - 3):
-                for j in range(1, OUT_BANKS):
-                    add_b1(step - 3, j)
             if is_unit(step + 2):
                 weave_rows(step + 2, range(0, 2), "x_ab")
                 weave_rows(step + 2, range(2, woven_rows(step + 2)), "x_cd")
             if step + 2 in PLAIN_UNITS:
                 turn_plain(step + 2)
                 copy_sample(step + 2)
+            if is_unit(step - 4):
+                finish(step - 4, 2)
             if is_unit(step - 3):
-                finish(step - 3, 0)
+                for j in range(OUT_BANKS):
+                    layer2(step - 3, j)
             for k in range(2 + 1, len(CHUNKS)):
                 if step == CHUNKS[k][0] - 2 * WOVEN_BUFS:
                     load_woven(k)

@@ -27,7 +27,7 @@ SETS = P // STREAMS
 H_BANKS = 2
 OUT_BANKS = 3
 PLAIN_LOAD = 2
-WOVEN_BUFS = 3
+WOVEN_BUFS = 2
 CHUNKS = [(0, 1), (1, 1)] + [(u, 2) for u in range(2, UNITS - 2, 2)] + [(UNITS - 2, 1), (UNITS - 1, 1)]
 
 
@@ -100,11 +100,17 @@ def tile_samplequerymessagepassing_pa_t_kernel(
             for u in range(PLAIN_LOAD):
                 live["plain", first + u] = plain[:, :, u * C : (u + 1) * C]
 
-        def clear(engine, i, sets):
-            engine.memset(woven_tiles[i][:].bitcast(U32)[:, sets, :], 0)
+        def clear(i):
+            nc.vector.memset(woven_tiles[i][:].bitcast(U32), 0)
 
-        clear(nc.vector, 0, slice(0, 2))
-        clear(nc.gpsimd, 0, slice(2, SETS))
+        zero = stage.tile([P, 1], U32)
+        nc.vector.memset(zero[:], 0)
+
+        def clear_by_scalar(i):
+            words = woven_tiles[i][:].rearrange("p r c -> p (r c)").bitcast(U32)
+            nc.scalar.copy(out=words, in_=zero[:].to_broadcast(words.shape))
+
+        clear(0)
         w0_raw = stage.tile([P, PACK, MID], BF16)
         nc.scalar.dma_start(out=w0_raw[:], in_=W0.rearrange("(t p) n -> p t n", p=P))
         b0_rows = stage.tile([P, P], BF16)
@@ -116,18 +122,19 @@ def tile_samplequerymessagepassing_pa_t_kernel(
         nc.scalar.activation(out=warm[:], in_=warm[:], func=ACT.Gelu_apprx_tanh)
         ident = keep.tile([P, P], BF16)
         make_identity(nc, ident[:])
-        clear(nc.vector, 1, slice(0, SETS))
+        clear(1)
         load_woven(1)
         load_plain(1)
         w1_raw = stage.tile([P, PACK, MID], BF16)
         nc.sync.dma_start(out=w1_raw[:], in_=W1.rearrange("(t p) n -> p t n", p=P))
         b1_rows = stage.tile([P, MID], BF16)
-        nc.gpsimd.memset(b1_rows[:].bitcast(U32), 0)
+        nc.vector.memset(b1_rows[:].bitcast(U32), 0)
         nc.sync.dma_start(out=b1_rows[0:1, :], in_=b1.rearrange("(o n) -> o n", o=1))
-        clear(nc.gpsimd, 2, slice(0, SETS))
+        clear_by_scalar(2)
         load_woven(2)
         load_plain(3)
 
+        clear_by_scalar(3)
         ident_f32 = keep.tile([P, P], F32)
         nc.vector.tensor_copy(out=ident_f32[:], in_=ident[:])
         weave = keep.tile([P, STREAMS, 2], BF16)
@@ -136,14 +143,6 @@ def tile_samplequerymessagepassing_pa_t_kernel(
         nc.vector.tensor_tensor(out=q_places[:], in0=places[:, :, 1], in1=places[:, :, 2], op=ALU.add)
         nc.vector.tensor_tensor(out=weave[:, :, 0], in0=places[:, :, 0], in1=q_places[:], op=ALU.subtract)
         nc.vector.tensor_scalar_mul(out=weave[:, :, 1], in0=q_places[:], scalar1=-1.0)
-        ones = stage.tile([P, P], BF16)
-        nc.vector.memset(ones[:], 1.0)
-
-        sample_t = []
-        for i in range(2):
-            sample_zero = keep.tile([P, 2, 2, P], BF16, name="sample_zero%d" % i)
-            nc.vector.memset(sample_zero[:, 1, :, :].rearrange("p c n -> p (c n)").bitcast(U32), 0)
-            sample_t.append(sample_zero)
 
         def quantise_weight(grouped, name):
             codes = keep.tile([P, MID], U32, name=name + "_codes", align_bytes=64)
@@ -163,16 +162,22 @@ def tile_samplequerymessagepassing_pa_t_kernel(
         )
         w0_codes, w0_scales = quantise_weight(w0_grouped, "w0")
 
+        sample_t = []
+        for i in range(2):
+            sample_zero = keep.tile([P, 2, 2, P], BF16, name="sample_zero%d" % i)
+            nc.vector.memset(sample_zero[:, 1, :, :].rearrange("p c n -> p (c n)").bitcast(U32), 0)
+            sample_t.append(sample_zero)
+
+        ones = stage.tile([P, P], BF16)
+        nc.vector.memset(ones[:], 1.0)
+
         b0_ps = ps_out.tile([P, MID], F32, tag="out_ps")
         b0_turned = b0_ps[:].bitcast(BF16)[:, 0:P]
         nc.tensor.transpose(b0_turned, b0_rows[:], ident[:])
         b0_cols = keep.tile([P, PACK], F32)
         nc.vector.tensor_copy(out=b0_cols[:], in_=b0_turned[:, 0:PACK])
 
-        grouped_tiles = []
-        for i in range(2):
-            grouped = keep.tile([P, 2, UNIT, PACK], BF16, name="grouped%d" % i, align_bytes=64)
-            grouped_tiles.append(grouped)
+        grouped = keep.tile([P, 2, UNIT, PACK], BF16, align_bytes=64)
         b1_all = keep.tile([P, MID], F32)
 
         def add_plain(unit):
@@ -218,20 +223,19 @@ def tile_samplequerymessagepassing_pa_t_kernel(
 
         def copy_x(unit, rows, name):
             tokens = slice(rows[0] * P, (rows[-1] + 1) * P)
-            nc.vector.tensor_copy(out=grouped_tiles[unit % 2][:, 0, tokens, :], in_=live[name, unit][:, 0 : len(rows) * P, :])
+            nc.vector.tensor_copy(out=grouped[:, 0, tokens, :], in_=live[name, unit][:, 0 : len(rows) * P, :])
 
         def make_plain_x(unit):
             tokens = slice((UNIT_ROWS - 1) * P, UNIT)
             q_ps = live["plain_ps", unit][0]
             nc.vector.tensor_tensor(
-                out=grouped_tiles[unit % 2][:, 0, tokens, :].rearrange("p n (c h) -> p n c h", h=2),
+                out=grouped[:, 0, tokens, :].rearrange("p n (c h) -> p n c h", h=2),
                 in0=sample_t[unit % 2][:].rearrange("p h c n -> p n c h"),
                 in1=q_ps.rearrange("p (c n) -> p n c", c=2).unsqueeze(3).to_broadcast([P, P, 2, 2]),
                 op=ALU.subtract,
             )
 
         def quantise(x_unit, h_unit):
-            grouped = grouped_tiles[x_unit % 2]
             first = 0 if is_unit(x_unit) else 1
             last = 2 if is_unit(h_unit) else 1
             codes = work.tile([P, 2, UNIT], U32, align_bytes=64)
@@ -250,7 +254,10 @@ def tile_samplequerymessagepassing_pa_t_kernel(
                 live["h_planes", unit] = h_planes
             x_codes, x_scales = live["x", unit]
             m_cols = slice(m * P, (m + 1) * P)
-            h_ps = ps_h.tile([P, UNIT], F32)
+            if unit < 2 and m >= H_BANKS:
+                h_ps = ps_out.tile([P, UNIT], F32, tag="out_ps")
+            else:
+                h_ps = ps_h.tile([P, UNIT], F32)
             nc.tensor.matmul_mx(
                 out=h_ps[:],
                 lhsT=w0_codes[:, m_cols].bitcast(FP8X4),
@@ -268,7 +275,10 @@ def tile_samplequerymessagepassing_pa_t_kernel(
                 scale=1.0,
             )
 
-        def lay_words(out, planes):
+        def lay_words(out, planes, by_vector=False):
+            if by_vector:
+                nc.vector.tensor_copy(out=out, in_=planes.rearrange("p t n -> p n t"))
+                return
             nc.gpsimd.tensor_scalar(
                 out=out,
                 in0=planes.rearrange("p t n -> p n t"),
@@ -280,7 +290,7 @@ def tile_samplequerymessagepassing_pa_t_kernel(
 
         def regroup_h(unit, half_unit):
             tokens = slice(half_unit * (UNIT // 2), (half_unit + 1) * (UNIT // 2))
-            lay_words(grouped_tiles[(unit + 1) % 2][:, 1, tokens, :], live["h_planes", unit][:, :, tokens])
+            lay_words(grouped[:, 1, tokens, :], live["h_planes", unit][:, :, tokens], unit in (0, 15))
 
         def layer2(unit, j):
             h_codes, h_scales = live["h", unit]
@@ -307,6 +317,15 @@ def tile_samplequerymessagepassing_pa_t_kernel(
             )
 
         def finish(unit, j0):
+            if unit == UNITS - 1 and j0 == 2:
+                for j in (2, 3):
+                    result1 = stores.tile([P, 1, MID], F32)
+                    nc.scalar.activation(out=result1[:], in_=live["biased", unit][:, j : j + 1, :], func=ACT.Gelu_apprx_tanh)
+                    nc.sync.dma_start(out=out_rows[:, row_of(unit, j) : row_of(unit, j) + 1, :], in_=result1[:])
+                return
+            finish2(unit, j0)
+
+        def finish2(unit, j0):
             result = stores.tile([P, 2, MID], F32)
             nc.scalar.activation(out=result[:], in_=live["biased", unit][:, j0 : j0 + 2, :], func=ACT.Gelu_apprx_tanh)
             row0, row1 = row_of(unit, j0), row_of(unit, j0 + 1)
@@ -315,7 +334,7 @@ def tile_samplequerymessagepassing_pa_t_kernel(
         w1_grouped = stage.tile([P, MID, PACK], BF16, align_bytes=64)
 
         def regroup_w1():
-            lay_words(w1_grouped[:], w1_raw[:])
+            nc.vector.tensor_copy(out=w1_grouped[:], in_=w1_raw[:].rearrange("p t n -> p n t"))
 
         def prepare_layer2():
             live["w1"] = quantise_weight(w1_grouped, "w1")
@@ -323,47 +342,46 @@ def tile_samplequerymessagepassing_pa_t_kernel(
             nc.tensor.matmul(out=b1_ps[:], lhsT=ones[:], rhs=b1_rows[:], start=True, stop=True)
             nc.vector.tensor_copy(out=b1_all[:], in_=b1_ps[:])
 
-        for step in range(-3, UNITS + 5):
-            if is_unit(step) or is_unit(step - 3):
-                quantise(step, step - 3)
-            if is_unit(step - 4):
-                for j in range(OUT_BANKS):
-                    add_b1(step - 4, j)
+        for step in range(-2, UNITS + 4):
+            if is_unit(step) or is_unit(step - 2):
+                quantise(step, step - 2)
+            if is_unit(step - 3):
+                add_b1(step - 3, OUT_BANKS)
             if is_unit(step + 1):
                 copy_x(step + 1, range(0, 2), "x_ab")
                 copy_x(step + 1, range(2, woven_rows(step + 1)), "x_cd")
+            if step + 1 in PLAIN_UNITS:
+                make_plain_x(step + 1)
             if is_unit(step - 1):
                 regroup_h(step - 1, 0)
                 regroup_h(step - 1, 1)
-            if step + 3 in PLAIN_UNITS:
-                add_plain(step + 3)
-            if step < -1:
-                clear(nc.gpsimd, step + 6, slice(0, SETS))
+            if step + 2 in PLAIN_UNITS:
+                add_plain(step + 2)
             for m in range(PACK):
-                if m == H_BANKS and is_unit(step - 4):
-                    layer2(step - 4, OUT_BANKS)
+                if m == H_BANKS and is_unit(step - 2):
+                    for j in range(OUT_BANKS):
+                        layer2(step - 2, j)
+                if m == H_BANKS and is_unit(step - 3):
+                    finish(step - 3, 2)
                 if is_unit(step):
                     layer1(step, m)
             if step == 0:
                 regroup_w1()
-            if step == 2:
+            if step == 1:
                 prepare_layer2()
-            if is_unit(step - 4):
-                finish(step - 4, 0)
-                add_b1(step - 4, OUT_BANKS)
-            if step + 1 in PLAIN_UNITS:
-                make_plain_x(step + 1)
+            if is_unit(step - 2):
+                add_b1(step - 2, 0)
+                layer2(step - 2, OUT_BANKS)
+            if is_unit(step - 2):
+                for j in range(1, OUT_BANKS):
+                    add_b1(step - 2, j)
+                finish(step - 2, 0)
             if is_unit(step + 2):
                 weave_rows(step + 2, range(0, 2), "x_ab")
                 weave_rows(step + 2, range(2, woven_rows(step + 2)), "x_cd")
             if step + 2 in PLAIN_UNITS:
                 turn_plain(step + 2)
                 copy_sample(step + 2)
-            if is_unit(step - 4):
-                finish(step - 4, 2)
-            if is_unit(step - 3):
-                for j in range(OUT_BANKS):
-                    layer2(step - 3, j)
             for k in range(2 + 1, len(CHUNKS)):
                 if step == CHUNKS[k][0] - 2 * WOVEN_BUFS:
                     load_woven(k)

@@ -20,7 +20,7 @@ ROWS = TOKENS // P
 UNIT_ROWS = 4
 UNIT = UNIT_ROWS * P
 UNITS = ROWS // UNIT_ROWS
-PLAIN_UNITS = range(1, UNITS - 1)
+PLAIN_UNITS = range(2, UNITS)
 STREAMS = 32
 WEAVE = 4
 SETS = P // STREAMS
@@ -28,7 +28,7 @@ H_BANKS = 2
 OUT_BANKS = 3
 PLAIN_LOAD = 2
 WOVEN_BUFS = 2
-CHUNKS = [(0, 1), (1, 1)] + [(u, 2) for u in range(2, UNITS - 2, 2)] + [(UNITS - 2, 1), (UNITS - 1, 1)]
+CHUNKS = [(0, 1), (1, 1)] + [(u, 2) for u in range(2, UNITS, 2)]
 
 
 def woven_rows(unit):
@@ -124,7 +124,7 @@ def tile_samplequerymessagepassing_pa_t_kernel(
         make_identity(nc, ident[:])
         clear(1)
         load_woven(1)
-        load_plain(1)
+        load_plain(2)
         w1_raw = stage.tile([P, PACK, MID], BF16)
         nc.sync.dma_start(out=w1_raw[:], in_=W1.rearrange("(t p) n -> p t n", p=P))
         b1_rows = stage.tile([P, MID], BF16)
@@ -132,7 +132,6 @@ def tile_samplequerymessagepassing_pa_t_kernel(
         nc.sync.dma_start(out=b1_rows[0:1, :], in_=b1.rearrange("(o n) -> o n", o=1))
         clear_by_scalar(2)
         load_woven(2)
-        load_plain(3)
 
         clear_by_scalar(3)
         ident_f32 = keep.tile([P, P], F32)
@@ -171,20 +170,24 @@ def tile_samplequerymessagepassing_pa_t_kernel(
         ones = stage.tile([P, P], BF16)
         nc.vector.memset(ones[:], 1.0)
 
-        b0_ps = ps_out.tile([P, MID], F32, tag="out_ps")
-        b0_turned = b0_ps[:].bitcast(BF16)[:, 0:P]
-        nc.tensor.transpose(b0_turned, b0_rows[:], ident[:])
         b0_cols = keep.tile([P, PACK], F32)
-        nc.vector.tensor_copy(out=b0_cols[:], in_=b0_turned[:, 0:PACK])
+
+        def turn_b0():
+            b0_ps = ps_out.tile([P, MID], F32, tag="out_ps")
+            b0_turned = b0_ps[:].bitcast(BF16)[:, 0:P]
+            nc.tensor.transpose(b0_turned, b0_rows[:], ident[:])
+            return b0_turned
 
         grouped = keep.tile([P, 2, UNIT, PACK], BF16, align_bytes=64)
         b1_all = keep.tile([P, MID], F32)
 
-        def add_plain(unit):
+        def add_plain(unit, c, add):
+            if c == 0:
+                q_row = work.tile([P, C], F32)
+                live["q_row", unit] = q_row
             plain = live["plain", unit]
-            q_row = work.tile([P, C], F32)
-            nc.gpsimd.tensor_tensor(out=q_row[:], in0=plain[:, 1, :], in1=plain[:, 2, :], op=ALU.add)
-            live["q_row", unit] = q_row
+            cols = slice(c * P, (c + 1) * P)
+            add(out=live["q_row", unit][:, cols], in0=plain[:, 1, cols], in1=plain[:, 2, cols], op=ALU.add)
 
         def turn_plain(unit):
             plain_ps = ps_x.tile([P, MID], F32)
@@ -288,9 +291,8 @@ def tile_samplequerymessagepassing_pa_t_kernel(
                 op1=ALU.add,
             )
 
-        def regroup_h(unit, half_unit):
-            tokens = slice(half_unit * (UNIT // 2), (half_unit + 1) * (UNIT // 2))
-            lay_words(grouped[:, 1, tokens, :], live["h_planes", unit][:, :, tokens], unit in (0, 15))
+        def regroup_h(unit):
+            lay_words(grouped[:, 1, :, :], live["h_planes", unit][:], unit in (0, 15))
 
         def layer2(unit, j):
             h_codes, h_scales = live["h", unit]
@@ -343,20 +345,25 @@ def tile_samplequerymessagepassing_pa_t_kernel(
             nc.vector.tensor_copy(out=b1_all[:], in_=b1_ps[:])
 
         for step in range(-2, UNITS + 4):
-            if is_unit(step) or is_unit(step - 2):
+            if is_unit(step) or is_unit(step - 2) and step <= UNITS:
                 quantise(step, step - 2)
+            if step + 2 in PLAIN_UNITS:
+                add_plain(step + 2, 0, nc.vector.tensor_tensor)
             if is_unit(step - 3):
                 add_b1(step - 3, OUT_BANKS)
             if is_unit(step + 1):
                 copy_x(step + 1, range(0, 2), "x_ab")
                 copy_x(step + 1, range(2, woven_rows(step + 1)), "x_cd")
+            if step == -1:
+                nc.vector.tensor_copy(out=b0_cols[:], in_=b0_turned[:, 0:PACK])
             if step + 1 in PLAIN_UNITS:
                 make_plain_x(step + 1)
             if is_unit(step - 1):
-                regroup_h(step - 1, 0)
-                regroup_h(step - 1, 1)
+                regroup_h(step - 1)
+            if step == UNITS:
+                quantise(-1, UNITS - 1)
             if step + 2 in PLAIN_UNITS:
-                add_plain(step + 2)
+                add_plain(step + 2, 1, nc.gpsimd.tensor_tensor)
             for m in range(PACK):
                 if m == H_BANKS and is_unit(step - 2):
                     for j in range(OUT_BANKS):
@@ -379,11 +386,13 @@ def tile_samplequerymessagepassing_pa_t_kernel(
             if is_unit(step + 2):
                 weave_rows(step + 2, range(0, 2), "x_ab")
                 weave_rows(step + 2, range(2, woven_rows(step + 2)), "x_cd")
+            if step == -2:
+                b0_turned = turn_b0()
             if step + 2 in PLAIN_UNITS:
                 turn_plain(step + 2)
                 copy_sample(step + 2)
             for k in range(2 + 1, len(CHUNKS)):
                 if step == CHUNKS[k][0] - 2 * WOVEN_BUFS:
                     load_woven(k)
-            if step >= -1 and step % 2 == 1 and step + 6 in PLAIN_UNITS:
+            if step >= -2 and step % 2 == 0 and step + 6 in PLAIN_UNITS:
                 load_plain(step + 6)

@@ -124,9 +124,9 @@ def tile_samplequerymessagepassing_pa_t_kernel(
         make_identity(nc, ident[:])
         clear(1)
         load_woven(1)
-        load_plain(2)
         w1_raw = stage.tile([P, PACK, MID], BF16)
         nc.sync.dma_start(out=w1_raw[:], in_=W1.rearrange("(t p) n -> p t n", p=P))
+        load_plain(2)
         b1_rows = stage.tile([P, MID], BF16)
         nc.vector.memset(b1_rows[:].bitcast(U32), 0)
         nc.sync.dma_start(out=b1_rows[0:1, :], in_=b1.rearrange("(o n) -> o n", o=1))
@@ -226,7 +226,8 @@ def tile_samplequerymessagepassing_pa_t_kernel(
 
         def copy_x(unit, rows, name):
             tokens = slice(rows[0] * P, (rows[-1] + 1) * P)
-            nc.vector.tensor_copy(out=grouped[:, 0, tokens, :], in_=live[name, unit][:, 0 : len(rows) * P, :])
+            copy = nc.scalar.copy if name == "x_cd" and unit > 1 and unit % 2 == 1 else nc.vector.tensor_copy
+            copy(out=grouped[:, 0, tokens, :], in_=live[name, unit][:, 0 : len(rows) * P, :])
 
         def make_plain_x(unit):
             tokens = slice((UNIT_ROWS - 1) * P, UNIT)
@@ -335,8 +336,7 @@ def tile_samplequerymessagepassing_pa_t_kernel(
 
         w1_grouped = stage.tile([P, MID, PACK], BF16, align_bytes=64)
 
-        def regroup_w1():
-            nc.vector.tensor_copy(out=w1_grouped[:], in_=w1_raw[:].rearrange("p t n -> p n t"))
+        nc.scalar.copy(out=w1_grouped[:], in_=w1_raw[:].rearrange("p t n -> p n t"))
 
         def prepare_layer2():
             live["w1"] = quantise_weight(w1_grouped, "w1")
@@ -349,6 +349,8 @@ def tile_samplequerymessagepassing_pa_t_kernel(
                 quantise(step, step - 2)
             if step + 2 in PLAIN_UNITS:
                 add_plain(step + 2, 0, nc.vector.tensor_tensor)
+            if step == 2:
+                prepare_layer2()
             if is_unit(step - 3):
                 add_b1(step - 3, OUT_BANKS)
             if is_unit(step + 1):
@@ -372,10 +374,6 @@ def tile_samplequerymessagepassing_pa_t_kernel(
                     finish(step - 3, 2)
                 if is_unit(step):
                     layer1(step, m)
-            if step == 0:
-                regroup_w1()
-            if step == 1:
-                prepare_layer2()
             if is_unit(step - 2):
                 add_b1(step - 2, 0)
                 layer2(step - 2, OUT_BANKS)

from contextlib import ExitStack

import concourse.mybir as mybir
from concourse.masks import make_identity

F32 = mybir.dt.float32
BF16 = mybir.dt.bfloat16
U32 = mybir.dt.uint32
U8 = mybir.dt.uint8
FP8X4 = mybir.dt.float8_e4m3fn_x4
ALU = mybir.AluOpType
ACT = mybir.ActivationFunctionType

P = 128
PACK = 4
TOKENS = 2 * 4096
C = 256
MID = 512
ROWS = TOKENS // P
UNIT_ROWS = 4
UNIT = UNIT_ROWS * P
UNITS = ROWS // UNIT_ROWS
PLAIN_UNITS = range(2, UNITS)
STREAMS = 32
WEAVE = 4
SETS = P // STREAMS
H_BANKS = 2
OUT_BANKS = 3
PLAIN_LOAD = 2
WOVEN_BUFS = 2
CHUNKS = [(0, 1), (1, 1)] + [(u, 2) for u in range(2, UNITS, 2)]


def woven_rows(unit):
    return UNIT_ROWS - (unit in PLAIN_UNITS)


def first_row(unit):
    return sum(woven_rows(u) for u in range(unit))


def row_of(unit, j):
    if j < woven_rows(unit):
        return first_row(unit) + j
    return first_row(UNITS) + PLAIN_UNITS.index(unit)


FLOPS = 2 * TOKENS * (2 * C * MID + MID * MID)


def tile_samplequerymessagepassing_pa_t_kernel(
    tc, sample_features, query_samples, pos_enc, W0, b0, W1, b1, out
):
    nc = tc.nc
    inputs = (sample_features, query_samples, pos_enc)
    woven_views = [
        x.rearrange("b s c -> (b s) c").rearrange("(r n row) c -> n r (row c)", r=SETS, n=STREAMS) for x in inputs
    ]
    plain_views = [x.rearrange("b s c -> (b s) c").rearrange("(p row) c -> p (row c)", p=P) for x in inputs]
    out_rows = out.rearrange("b s m -> (b s) m").rearrange("(p r) m -> p r m", p=P)

    with ExitStack() as ctx:
        ctx.enter_context(tc.manual_schedule())
        keep = ctx.enter_context(tc.tile_pool(name="keep", bufs=1))
        stage = ctx.enter_context(tc.tile_pool(name="stage", bufs=1))
        loads = ctx.enter_context(tc.tile_pool(name="loads", bufs=3))
        work = ctx.enter_context(tc.tile_pool(name="work", bufs=4))
        stores = ctx.enter_context(tc.tile_pool(name="stores", bufs=6))
        ps_x = ctx.enter_context(tc.psum_pool(name="ps_x", bufs=1))
        ps_h = ctx.enter_context(tc.psum_pool(name="ps_h", bufs=H_BANKS))
        ps_out = ctx.enter_context(tc.psum_pool(name="ps_out", bufs=OUT_BANKS))

        live = {}

        def is_unit(unit):
            return 0 <= unit < UNITS

        woven_tiles = []
        for i in range(2 + WOVEN_BUFS):
            first, count = CHUNKS[i]
            rows = first_row(first + count) - first_row(first)
            woven = keep.tile([P, SETS, rows * C], BF16, name="woven%d" % i)
            woven_tiles.append(woven)

        def load_woven(k):
            first, count = CHUNKS[k]
            woven = woven_tiles[k if k < 2 else 2 + (k - 2) % WOVEN_BUFS]
            start, stop = first_row(first) * C, first_row(first + count) * C
            for i in range(3):
                nc.sync.dma_start(out=woven[i:P:WEAVE, :, 0 : stop - start], in_=woven_views[i][:, :, start:stop])
            for u in range(first, first + count):
                live["woven", u] = (woven, first_row(u) * C - start)

        def load_plain(first):
            plain = loads.tile([P, 3, PLAIN_LOAD * C], BF16)
            start = row_of(first, UNIT_ROWS - 1) * C
            cols = slice(start, start + PLAIN_LOAD * C)
            for i in range(3):
                nc.sync.dma_start(out=plain[:, i, :], in_=plain_views[i][:, cols])
            for u in range(PLAIN_LOAD):
                live["plain", first + u] = plain[:, :, u * C : (u + 1) * C]

        def clear(i):
            nc.vector.memset(woven_tiles[i][:].bitcast(U32), 0)

        zero = stage.tile([P, 1], U32)
        nc.vector.memset(zero[:], 0)

        def clear_by_scalar(i):
            words = woven_tiles[i][:].rearrange("p r c -> p (r c)").bitcast(U32)
            nc.scalar.copy(out=words, in_=zero[:].to_broadcast(words.shape))

        clear(0)
        w0_raw = stage.tile([P, PACK, MID], BF16)
        nc.scalar.dma_start(out=w0_raw[:], in_=W0.rearrange("(t p) n -> p t n", p=P))
        b0_rows = stage.tile([P, P], BF16)
        nc.vector.memset(b0_rows[:].bitcast(U32), 0)
        nc.scalar.dma_start(out=b0_rows[0:PACK, :], in_=b0.rearrange("(m p) -> m p", p=P))
        load_woven(0)
        warm = stage.tile([P, 1], F32)
        nc.vector.memset(warm[:], 0.0)
        nc.scalar.activation(out=warm[:], in_=warm[:], func=ACT.Gelu_apprx_tanh)
        ident = keep.tile([P, P], BF16)
        make_identity(nc, ident[:])
        clear(1)
        load_woven(1)
        w1_raw = stage.tile([P, PACK, MID], BF16)
        nc.sync.dma_start(out=w1_raw[:], in_=W1.rearrange("(t p) n -> p t n", p=P))
        load_plain(2)
        b1_rows = stage.tile([P, MID], BF16)
        nc.vector.memset(b1_rows[:].bitcast(U32), 0)
        nc.sync.dma_start(out=b1_rows[0:1, :], in_=b1.rearrange("(o n) -> o n", o=1))
        clear_by_scalar(2)
        load_woven(2)

        clear_by_scalar(3)
        ident_f32 = keep.tile([P, P], F32)
        nc.vector.tensor_copy(out=ident_f32[:], in_=ident[:])
        weave = keep.tile([P, STREAMS, 2], BF16)
        places = ident[:].rearrange("k (n i) -> k n i", i=WEAVE)
        q_places = stage.tile([P, STREAMS], BF16)
        nc.vector.tensor_tensor(out=q_places[:], in0=places[:, :, 1], in1=places[:, :, 2], op=ALU.add)
        nc.vector.tensor_tensor(out=weave[:, :, 0], in0=places[:, :, 0], in1=q_places[:], op=ALU.subtract)
        nc.vector.tensor_scalar_mul(out=weave[:, :, 1], in0=q_places[:], scalar1=-1.0)

        def quantise_weight(grouped, name):
            codes = keep.tile([P, MID], U32, name=name + "_codes", align_bytes=64)
            scales = keep.tile([P, MID], U8, name=name + "_scales", align_bytes=64)
            nc.vector.quantize_mx(
                out=codes[:].bitcast(FP8X4),
                scales=scales[:],
                in_=grouped[:].rearrange("p n t -> p (n t)"),
            )
            return codes, scales

        nc.vector.tensor_scalar_mul(out=w0_raw[:, 2:4, :], in0=w0_raw[:, 2:4, :], scalar1=-1.0)
        w0_grouped = stage.tile([P, MID, PACK], BF16, align_bytes=64)
        nc.vector.tensor_copy(
            out=w0_grouped[:].rearrange("p n (c h) -> p n c h", h=2),
            in_=w0_raw[:].rearrange("p (h c) n -> p n c h", h=2),
        )
        w0_codes, w0_scales = quantise_weight(w0_grouped, "w0")

        sample_t = []
        for i in range(2):
            sample_zero = keep.tile([P, 2, 2, P], BF16, name="sample_zero%d" % i)
            nc.vector.memset(sample_zero[:, 1, :, :].rearrange("p c n -> p (c n)").bitcast(U32), 0)
            sample_t.append(sample_zero)

        ones = stage.tile([P, P], BF16)
        nc.vector.memset(ones[:], 1.0)

        b0_cols = keep.tile([P, PACK], F32)

        def turn_b0():
            b0_ps = ps_out.tile([P, MID], F32, tag="out_ps")
            b0_turned = b0_ps[:].bitcast(BF16)[:, 0:P]
            nc.tensor.transpose(b0_turned, b0_rows[:], ident[:])
            return b0_turned

        grouped = keep.tile([P, 2, UNIT, PACK], BF16, align_bytes=64)
        b1_all = keep.tile([P, MID], F32)

        def add_plain(unit, c, add):
            if c == 0:
                q_row = work.tile([P, C], F32)
                live["q_row", unit] = q_row
            plain = live["plain", unit]
            cols = slice(c * P, (c + 1) * P)
            add(out=live["q_row", unit][:, cols], in0=plain[:, 1, cols], in1=plain[:, 2, cols], op=ALU.add)

        def turn_plain(unit):
            plain_ps = ps_x.tile([P, MID], F32)
            q_ps = plain_ps[:, 0:C]
            sample_ps = plain_ps[:, C : C + P].bitcast(BF16)
            for c in range(2):
                cols = slice(c * P, (c + 1) * P)
                nc.tensor.transpose(q_ps[:, cols], live["q_row", unit][:, cols], ident_f32[:])
            for c in range(2):
                cols = slice(c * P, (c + 1) * P)
                nc.tensor.transpose(sample_ps[:, cols], live["plain", unit][:, 0, cols], ident[:])
            live["plain_ps", unit] = (q_ps, sample_ps)

        def copy_sample(unit):
            sample_ps = live["plain_ps", unit][1]
            nc.scalar.copy(
                out=sample_t[unit % 2][:, 0, :, :], in_=sample_ps.rearrange("p (c n) -> p c n", c=2)
            )

        def weave_rows(unit, rows, name):
            woven, start = live["woven", unit]
            x_ps = ps_x.tile([P, 2 * P, PACK], BF16, name=name, tag=name)
            for jj, j in enumerate(rows):
                for r in range(SETS):
                    n0 = jj * P + r * STREAMS
                    for c in range(2):
                        first = start + j * C + c * P
                        nc.tensor.matmul(
                            out=x_ps[:, n0 : n0 + STREAMS, 2 * c : 2 * c + 2],
                            lhsT=woven[:, r, first : first + P],
                            rhs=weave[:],
                            start=True,
                            stop=True,
                        )
            live[name, unit] = x_ps

        def copy_x(unit, rows, name):
            tokens = slice(rows[0] * P, (rows[-1] + 1) * P)
            copy = nc.scalar.copy if name == "x_cd" and unit > 1 and unit % 2 == 1 else nc.vector.tensor_copy
            copy(out=grouped[:, 0, tokens, :], in_=live[name, unit][:, 0 : len(rows) * P, :])

        def make_plain_x(unit):
            tokens = slice((UNIT_ROWS - 1) * P, UNIT)
            q_ps = live["plain_ps", unit][0]
            nc.vector.tensor_tensor(
                out=grouped[:, 0, tokens, :].rearrange("p n (c h) -> p n c h", h=2),
                in0=sample_t[unit % 2][:].rearrange("p h c n -> p n c h"),
                in1=q_ps.rearrange("p (c n) -> p n c", c=2).unsqueeze(3).to_broadcast([P, P, 2, 2]),
                op=ALU.subtract,
            )

        def quantise(x_unit, h_unit):
            first = 0 if is_unit(x_unit) else 1
            last = 2 if is_unit(h_unit) else 1
            codes = work.tile([P, 2, UNIT], U32, align_bytes=64)
            scales = work.tile([P, 2, UNIT], U8, align_bytes=64)
            nc.vector.quantize_mx(
                out=codes[:, first:last, :].rearrange("p g n -> p (g n)").bitcast(FP8X4),
                scales=scales[:, first:last, :].rearrange("p g n -> p (g n)"),
                in_=grouped[:, first:last, :, :].rearrange("p g n t -> p (g n t)"),
            )
            live["x", x_unit] = (codes[:, 0, :], scales[:, 0, :])
            live["h", h_unit] = (codes[:, 1, :], scales[:, 1, :])

        def layer1(unit, m):
            if m == 0:
                h_planes = work.tile([P, PACK, UNIT], BF16)
                live["h_planes", unit] = h_planes
            x_codes, x_scales = live["x", unit]
            m_cols = slice(m * P, (m + 1) * P)
            if unit < 2 and m >= H_BANKS:
                h_ps = ps_out.tile([P, UNIT], F32, tag="out_ps")
            else:
                h_ps = ps_h.tile([P, UNIT], F32)
            nc.tensor.matmul_mx(
                out=h_ps[:],
                lhsT=w0_codes[:, m_cols].bitcast(FP8X4),
                lhsT_scale=w0_scales[:, m_cols],
                rhs=x_codes.bitcast(FP8X4),
                rhs_scale=x_scales,
                start=True,
                stop=True,
            )
            nc.scalar.activation(
                out=live["h_planes", unit][:, m, :],
                in_=h_ps[:],
                func=ACT.Gelu_apprx_tanh,
                bias=b0_cols[:, m : m + 1],
                scale=1.0,
            )

        def lay_words(out, planes, by_vector=False):
            if by_vector:
                nc.vector.tensor_copy(out=out, in_=planes.rearrange("p t n -> p n t"))
                return
            nc.gpsimd.tensor_scalar(
                out=out,
                in0=planes.rearrange("p t n -> p n t"),
                scalar1=1.0,
                scalar2=0.0,
                op0=ALU.mult,
                op1=ALU.add,
            )

        def regroup_h(unit):
            lay_words(grouped[:, 1, :, :], live["h_planes", unit][:], unit in (0, 15))

        def layer2(unit, j):
            h_codes, h_scales = live["h", unit]
            w1_codes, w1_scales = live["w1"]
            j_cols = slice(j * P, (j + 1) * P)
            out_ps = ps_out.tile([P, MID], F32)
            nc.tensor.matmul_mx(
                out=out_ps[:],
                lhsT=h_codes[:, j_cols].bitcast(FP8X4),
                lhsT_scale=h_scales[:, j_cols],
                rhs=w1_codes[:].bitcast(FP8X4),
                rhs_scale=w1_scales[:],
                start=True,
                stop=True,
            )
            live["out_ps", unit, j] = out_ps

        def add_b1(unit, j):
            if j == 0:
                biased = work.tile([P, UNIT_ROWS, MID], F32)
                live["biased", unit] = biased
            nc.vector.tensor_tensor(
                out=live["biased", unit][:, j, :], in0=live["out_ps", unit, j][:], in1=b1_all[:], op=ALU.add
            )

        def finish(unit, j0):
            if unit == UNITS - 1 and j0 == 2:
                for j in (2, 3):
                    result1 = stores.tile([P, 1, MID], F32)
                    nc.scalar.activation(out=result1[:], in_=live["biased", unit][:, j : j + 1, :], func=ACT.Gelu_apprx_tanh)
                    nc.sync.dma_start(out=out_rows[:, row_of(unit, j) : row_of(unit, j) + 1, :], in_=result1[:])
                return
            finish2(unit, j0)

        def finish2(unit, j0):
            result = stores.tile([P, 2, MID], F32)
            nc.scalar.activation(out=result[:], in_=live["biased", unit][:, j0 : j0 + 2, :], func=ACT.Gelu_apprx_tanh)
            row0, row1 = row_of(unit, j0), row_of(unit, j0 + 1)
            nc.sync.dma_start(out=out_rows[:, row0 : row1 + 1 : row1 - row0, :], in_=result[:])

        w1_grouped = stage.tile([P, MID, PACK], BF16, align_bytes=64)

        nc.scalar.copy(out=w1_grouped[:], in_=w1_raw[:].rearrange("p t n -> p n t"))

        def prepare_layer2():
            live["w1"] = quantise_weight(w1_grouped, "w1")
            b1_ps = ps_out.tile([P, MID], F32, tag="out_ps")
            nc.tensor.matmul(out=b1_ps[:], lhsT=ones[:], rhs=b1_rows[:], start=True, stop=True)
            nc.vector.tensor_copy(out=b1_all[:], in_=b1_ps[:])

        for step in range(-2, UNITS + 4):
            if is_unit(step) or is_unit(step - 2) and step <= UNITS:
                quantise(step, step - 2)
            if step + 2 in PLAIN_UNITS:
                add_plain(step + 2, 0, nc.vector.tensor_tensor)
            if step == 2:
                prepare_layer2()
            if is_unit(step - 3):
                add_b1(step - 3, OUT_BANKS)
            if is_unit(step + 1):
                copy_x(step + 1, range(0, 2), "x_ab")
                copy_x(step + 1, range(2, woven_rows(step + 1)), "x_cd")
            if step == -1:
                nc.vector.tensor_copy(out=b0_cols[:], in_=b0_turned[:, 0:PACK])
            if step + 1 in PLAIN_UNITS:
                make_plain_x(step + 1)
            if is_unit(step - 1):
                regroup_h(step - 1)
            if step == UNITS:
                quantise(-1, UNITS - 1)
            if step + 2 in PLAIN_UNITS:
                add_plain(step + 2, 1, nc.gpsimd.tensor_tensor)
            for m in range(PACK):
                if m == H_BANKS and is_unit(step - 2):
                    for j in range(OUT_BANKS):
                        layer2(step - 2, j)
                if m == H_BANKS and is_unit(step - 3):
                    finish(step - 3, 2)
                if is_unit(step):
                    layer1(step, m)
            if is_unit(step - 2):
                add_b1(step - 2, 0)
                layer2(step - 2, OUT_BANKS)
            if is_unit(step - 2):
                for j in range(1, OUT_BANKS):
                    add_b1(step - 2, j)
                finish(step - 2, 0)
            if is_unit(step + 2):
                weave_rows(step + 2, range(0, 2), "x_ab")
                weave_rows(step + 2, range(2, woven_rows(step + 2)), "x_cd")
            if step == -2:
                b0_turned = turn_b0()
            if step + 2 in PLAIN_UNITS:
                turn_plain(step + 2)
                copy_sample(step + 2)
            for k in range(2 + 1, len(CHUNKS)):
                if step == CHUNKS[k][0] - 2 * WOVEN_BUFS:
                    load_woven(k)
            if step >= -2 and step % 2 == 0 and step + 6 in PLAIN_UNITS:
                load_plain(step + 6)
